import numpy as np
import ml_dtypes


def mxq(x, axis, fmt="e4m3"):
    dtype, down = {"e4m3": (ml_dtypes.float8_e4m3fn, 7), "e5m2": (ml_dtypes.float8_e5m2, 14)}[fmt]
    v = np.moveaxis(np.asarray(x, np.float32).astype(ml_dtypes.bfloat16).astype(np.float64), axis, -1)
    blocks = v.reshape(v.shape[:-1] + (-1, 32))
    amax = np.abs(blocks).max(-1, keepdims=True)
    byte = np.maximum(np.where(amax > 0, np.frexp(amax)[1] - 1 + 127, 0) - down, 1)
    scale = np.exp2(byte - 127.0)
    codes = (blocks / scale).astype(np.float32).astype(dtype).astype(np.float64)
    return np.moveaxis((codes * scale).reshape(v.shape), -1, axis)


WIDE = False


def mx_kscale(k):
    if not WIDE:
        return np.ones(k)
    levels = np.array([10, -10, 5, -5, 0])
    if k % 512:
        return np.exp2(np.random.permutation(np.resize(levels, k // 32))).repeat(32)
    a = np.empty((k // 512, 16))
    for p in range(k // 512):
        a[p, :8] = np.random.permutation(np.resize(levels, 8))
        for g in range(8):
            far = levels[np.abs(levels - a[p, g]) >= 10]
            a[p, g + 8] = far[np.random.randint(len(far))]
    return np.exp2(a.ravel()).repeat(32)


BF16 = ml_dtypes.bfloat16


def bf(x):
    return np.asarray(x, np.float32).astype(BF16)


def f64(x):
    return np.asarray(x).astype(np.float64)


B, N, DIN, DH, DOUT = 4096, 8, 64, 64, 64
KH = N * DH
KO = N * DOUT
EPS = 1e-5


def elu(v):
    return np.where(v > 0.0, v, np.expm1(np.minimum(v, 0.0)))


def sigmoid(v):
    return 1.0 / (1.0 + np.exp(-v))


def setup_inputs():
    rn = np.random.standard_normal
    s, t = mx_kscale(KH), mx_kscale(KO)
    return {
        "h": bf(elu(rn((B, KH))) * s),
        "x": bf(rn((B, N, DIN)) + 0.5),
        "cW1": bf(rn((KH, KO)) * 1.2 / np.sqrt(KH) / s[:, None] * t),
        "cb1": bf(rn(KO) * 0.3 * t),
        "cW4": bf(rn((KO, KO)) / np.sqrt(KO) / t[:, None]),
        "cb4": bf(rn(KO) * 0.3),
        "cW5": bf(rn((KO, KO)) / np.sqrt(KO) / t[:, None]),
        "cb5": bf(rn(KO) * 0.3),
        "clng": bf(1.0 + 0.2 * rn(KO)),
        "clnb": bf(0.2 * rn(KO)),
    }


def reference(h, x, cW1, cb1, cW4, cb4, cW5, cb5, clng, clnb):
    flat = f64(x).reshape(B, N * DIN)
    e1 = (mxq(f64(h), 1, "e4m3") @ mxq(f64(cW1), 0, "e4m3")) + f64(cb1)
    e1q = mxq(e1, 1, "e4m3")
    g = sigmoid((e1q @ mxq(f64(cW4), 0, "e4m3")) + f64(cb4)) * ((e1q @ mxq(f64(cW5), 0, "e4m3")) + f64(cb5))
    r = flat + g
    c = (r - r.mean(-1, keepdims=True)) * (1.0 / np.sqrt(r.var(-1, keepdims=True) + EPS)) * f64(clng) + f64(clnb)
    c = c.reshape(B, N, DOUT)
    e = np.exp(c - c.max(1, keepdims=True))
    return e / e.sum(1, keepdims=True)

@@ -1,0 +1,335 @@
+from contextlib import ExitStack
+
+import concourse.mybir as mybir
+from concourse.masks import make_identity
+
+F32 = mybir.dt.float32
+BF16 = mybir.dt.bfloat16
+U32 = mybir.dt.uint32
+U8 = mybir.dt.uint8
+FP8X4 = mybir.dt.float8_e4m3fn_x4
+ALU = mybir.AluOpType
+ACT = mybir.ActivationFunctionType
+
+P = 128
+PACK = 4
+B = 4096
+WIDTH = 512
+N_VAR = 8
+D_FEAT = 64
+CHUNK = 512
+ROW_TILES = CHUNK // P
+FEAT_TILES = WIDTH // P
+N_CHUNKS = B // CHUNK
+EPS = 1e-5
+
+FLOPS = 3 * 2 * B * WIDTH * WIDTH
+
+
+def tile_variableselectionnetwork_pa_t_kernel(
+    tc, h, x, cW1, cb1, cW4, cb4, cW5, cb5, clng, clnb, out
+):
+    nc = tc.nc
+    with ExitStack() as ctx:
+        consts = ctx.enter_context(tc.tile_pool(name="consts", bufs=1))
+        setup = ctx.enter_context(tc.tile_pool(name="setup", bufs=1))
+        io = ctx.enter_context(tc.tile_pool(name="io", bufs=3))
+        work = ctx.enter_context(tc.tile_pool(name="work", bufs=2))
+        gate = ctx.enter_context(tc.tile_pool(name="gate", bufs=2))
+        tail = ctx.enter_context(tc.tile_pool(name="tail", bufs=2))
+        psum = ctx.enter_context(tc.psum_pool(name="psum", bufs=2))
+
+        def load_chunk(c):
+            rows = slice(c * CHUNK, (c + 1) * CHUNK)
+            h_sb = io.tile([P, ROW_TILES, WIDTH], BF16, name="h_sb", tag="h_sb")
+            nc.sync.dma_start(out=h_sb[:], in_=h[rows, :].rearrange("(p a) k -> p a k", a=ROW_TILES))
+            x_sb = io.tile([P, ROW_TILES, WIDTH], BF16, name="x_sb", tag="x_sb")
+            nc.sync.dma_start(
+                out=x_sb[:], in_=x[rows, :, :].rearrange("(p a) n d -> p a (n d)", a=ROW_TILES)
+            )
+            return h_sb, x_sb
+
+        w1_raw = setup.tile([P, PACK, WIDTH], BF16, name="w1_raw")
+        nc.sync.dma_start(out=w1_raw[:], in_=cW1.rearrange("(p t) c -> p t c", t=PACK))
+        loaded = {0: load_chunk(0)}
+        cb1_raw = setup.tile([P, PACK], BF16, name="cb1_raw")
+        nc.sync.dma_start(out=cb1_raw[:], in_=cb1.rearrange("(p t) -> p t", t=PACK))
+        bias_rows = setup.tile([P, P], BF16, name="bias_rows")
+        nc.vector.memset(bias_rows[:], 0.0)
+        for i, vec in enumerate((cb4, cb5)):
+            nc.sync.dma_start(
+                out=bias_rows[FEAT_TILES * i : FEAT_TILES * (i + 1), :],
+                in_=vec.rearrange("(t p) -> t p", p=P),
+            )
+        w4_raw = setup.tile([P, PACK, WIDTH], BF16, name="w4_raw")
+        nc.sync.dma_start(out=w4_raw[:], in_=cW4.rearrange("(p t) c -> p t c", t=PACK))
+        w5_raw = setup.tile([P, PACK, WIDTH], BF16, name="w5_raw")
+        nc.sync.dma_start(out=w5_raw[:], in_=cW5.rearrange("(p t) c -> p t c", t=PACK))
+        clng_bc = consts.tile([P, WIDTH], BF16, name="clng_bc")
+        nc.gpsimd.dma_start(out=clng_bc[:], in_=clng.partition_broadcast(P))
+        clnb_bc = consts.tile([P, WIDTH], BF16, name="clnb_bc")
+        nc.gpsimd.dma_start(out=clnb_bc[:], in_=clnb.partition_broadcast(P))
+
+        ident_f32 = consts.tile([P, P], F32, name="ident_f32")
+        make_identity(nc, ident_f32[:])
+        ident_bf16 = consts.tile([P, P], BF16, name="ident_bf16")
+        make_identity(nc, ident_bf16[:])
+        swap_f32 = consts.tile([P, P], F32, name="swap_f32")
+        nc.vector.tensor_copy(out=swap_f32[:, 0:D_FEAT], in_=ident_f32[:, D_FEAT:P])
+        nc.vector.tensor_copy(out=swap_f32[:, D_FEAT:P], in_=ident_f32[:, 0:D_FEAT])
+        neg_half = consts.tile([P, ROW_TILES], F32, name="neg_half")
+        nc.vector.memset(neg_half[:], -0.5)
+
+        def quantise_weight(raw, copy, name, permute):
+            grouped = setup.tile([P, WIDTH, PACK], BF16, name=name + "_grouped", align_bytes=64)
+            if permute:
+                copy(
+                    out=grouped[:].rearrange("p (i m) t -> p i m t", i=PACK),
+                    in_=raw[:].rearrange("p t (m i) -> p i m t", i=PACK),
+                )
+            else:
+                copy(
+                    out=grouped[:].rearrange("p (c i) t -> p c t i", i=4),
+                    in_=raw[:].rearrange("p t (c i) -> p c t i", i=4),
+                )
+            codes = consts.tile([P, WIDTH], U32, name=name + "_codes", align_bytes=64)
+            scales = consts.tile([P, WIDTH], U8, name=name + "_scales", align_bytes=64)
+            nc.vector.quantize_mx(
+                out=codes[:].bitcast(FP8X4),
+                scales=scales[:],
+                in_=grouped[:].rearrange("p c t -> p (c t)"),
+            )
+            return codes, scales
+
+        w1_codes, w1_scales = quantise_weight(w1_raw, nc.vector.tensor_copy, "w1", True)
+        w4_codes, w4_scales = quantise_weight(w4_raw, nc.scalar.copy, "w4", False)
+        w5_codes, w5_scales = quantise_weight(w5_raw, nc.scalar.copy, "w5", False)
+
+        cb1_cols = consts.tile([P, PACK], F32, name="cb1_cols")
+        nc.vector.tensor_copy(out=cb1_cols[:], in_=cb1_raw[:])
+        bias_ps = psum.tile([P, P], BF16, name="bias_ps", tag="hT_ps", bufs=1)
+        nc.tensor.transpose(bias_ps[:], bias_rows[:], ident_bf16[:])
+        half_cb45_cols = consts.tile([P, 2 * FEAT_TILES], F32, name="half_cb45_cols")
+        nc.vector.tensor_scalar_mul(out=half_cb45_cols[:], in0=bias_ps[:, 0 : 2 * FEAT_TILES], scalar1=0.5)
+        half_cb4_cols = half_cb45_cols[:, 0:FEAT_TILES]
+        half_cb5_cols = half_cb45_cols[:, FEAT_TILES : 2 * FEAT_TILES]
+
+        def max_over_variables(src):
+            width = WIDTH
+            while width > D_FEAT:
+                width //= 2
+                dst = tail.tile([P, ROW_TILES, width], BF16, name="c_max_%d" % width)
+                nc.vector.tensor_tensor(
+                    out=dst[:], in0=src[:, :, 0:width], in1=src[:, :, width : 2 * width], op=ALU.max
+                )
+                src = dst
+            return src
+
+        def over_variables(per_feature):
+            return per_feature.unsqueeze(2).to_broadcast([P, ROW_TILES, N_VAR, D_FEAT])
+
+        def by_variable(tile_ap):
+            return tile_ap.rearrange("p a (n d) -> p a n d", n=N_VAR)
+
+        def chunk_to_exponentials(c):
+            if c + 1 < N_CHUNKS:
+                loaded[c + 1] = load_chunk(c + 1)
+            h_sb, x_sb = loaded[c]
+
+            h_grouped = work.tile([P, CHUNK * PACK], BF16, name="h_grouped", align_bytes=64)
+            h_grouped_words = h_grouped[:].bitcast(F32).rearrange(
+                "q (a b u) -> q a b u", a=ROW_TILES, u=2
+            )
+            for pair in range(ROW_TILES // 2):
+                hT_ps = psum.tile([P, 2, 2, P], F32, name="hT_ps", tag="hT_ps", bufs=1)
+                for a in range(2):
+                    h_words = h_sb[:, 2 * pair + a, :].bitcast(F32)
+                    for u in range(2):
+                        nc.tensor.transpose(
+                            hT_ps[:, a, u, :], h_words[:, u : 2 * P : 2], ident_f32[:]
+                        )
+                nc.scalar.copy(
+                    out=h_grouped_words[:, 2 * pair : 2 * pair + 2, :, :],
+                    in_=hT_ps[:].rearrange("q a u b -> q a b u"),
+                )
+            h_codes = work.tile([P, CHUNK], U32, name="h_codes", align_bytes=64)
+            h_scales = work.tile([P, CHUNK], U8, name="h_scales", align_bytes=64)
+            nc.vector.quantize_mx(out=h_codes[:].bitcast(FP8X4), scales=h_scales[:], in_=h_grouped[:])
+
+            e1_grouped = work.tile([P, CHUNK, PACK], BF16, name="e1_grouped", align_bytes=64)
+            for a in range(ROW_TILES):
+                cols = slice(a * P, (a + 1) * P)
+                e1_ps = psum.tile([P, PACK, P], F32, name="e1_ps", tag="e1_ps")
+                for t in range(PACK):
+                    feats = slice(t * P, (t + 1) * P)
+                    nc.tensor.matmul_mx(
+                        out=e1_ps[:, t, :],
+                        lhsT=w1_codes[:, feats].bitcast(FP8X4),
+                        lhsT_scale=w1_scales[:, feats],
+                        rhs=h_codes[:, cols].bitcast(FP8X4),
+                        rhs_scale=h_scales[:, cols],
+                        start=True,
+                        stop=True,
+                    )
+                nc.vector.tensor_tensor(
+                    out=e1_grouped[:, cols, :],
+                    in0=e1_ps[:].rearrange("p t b -> p b t"),
+                    in1=cb1_cols[:].unsqueeze(1).to_broadcast([P, P, PACK]),
+                    op=ALU.add,
+                )
+            e1_codes = work.tile([P, CHUNK], U32, name="e1_codes", align_bytes=64)
+            e1_scales = work.tile([P, CHUNK], U8, name="e1_scales", align_bytes=64)
+            nc.vector.quantize_mx(
+                out=e1_codes[:].bitcast(FP8X4),
+                scales=e1_scales[:],
+                in_=e1_grouped[:].rearrange("p b t -> p (b t)"),
+            )
+
+            gT = gate.tile([P, FEAT_TILES, CHUNK], F32, name="gT")
+            for j2 in range(0, FEAT_TILES, 2):
+                tanh_sb = gate.tile([P, 2, CHUNK], F32, name="tanh_sb")
+                half_lin_sb = gate.tile([P, 2, CHUNK], F32, name="half_lin_sb")
+                for i in range(2):
+                    j = j2 + i
+                    feats = slice(j * P, (j + 1) * P)
+                    u4_ps = psum.tile([P, CHUNK], F32, name="u4_ps", tag="u_ps")
+                    u5_ps = psum.tile([P, CHUNK], F32, name="u5_ps", tag="u_ps")
+                    for u_ps, codes, scales in ((u4_ps, w4_codes, w4_scales), (u5_ps, w5_codes, w5_scales)):
+                        nc.tensor.matmul_mx(
+                            out=u_ps[:],
+                            lhsT=codes[:, feats].bitcast(FP8X4),
+                            lhsT_scale=scales[:, feats],
+                            rhs=e1_codes[:].bitcast(FP8X4),
+                            rhs_scale=e1_scales[:],
+                            start=True,
+                            stop=True,
+                        )
+                    nc.scalar.activation(
+                        out=tanh_sb[:, i, :], in_=u4_ps[:], func=ACT.Tanh, bias=half_cb4_cols[:, j : j + 1], scale=0.5
+                    )
+                    nc.scalar.activation(
+                        out=half_lin_sb[:, i, :],
+                        in_=u5_ps[:],
+                        func=ACT.Identity,
+                        bias=half_cb5_cols[:, j : j + 1],
+                        scale=0.5,
+                    )
+                nc.vector.scalar_tensor_tensor(
+                    out=gT[:, j2 : j2 + 2, :], in0=tanh_sb[:], scalar=1.0, in1=half_lin_sb[:], op0=ALU.add, op1=ALU.mult
+                )
+
+            r_sb = tail.tile([P, ROW_TILES, WIDTH], F32, name="r_sb")
+            r_sum = tail.tile([P, ROW_TILES], F32, name="r_sum")
+            for a in range(ROW_TILES):
+                r_ps = psum.tile([P, WIDTH], F32, name="r_ps", tag="r_ps")
+                for j in range(FEAT_TILES):
+                    feats = slice(j * P, (j + 1) * P)
+                    nc.tensor.matmul(
+                        out=r_ps[:, feats], lhsT=ident_bf16[:], rhs=x_sb[:, a, feats], start=True, stop=False
+                    )
+                    nc.tensor.matmul(
+                        out=r_ps[:, feats],
+                        lhsT=gT[:, j, a * P : (a + 1) * P],
+                        rhs=ident_f32[:],
+                        start=False,
+                        stop=True,
+                        is_transpose=True,
+                    )
+                nc.scalar.activation(
+                    out=r_sb[:, a, :], in_=r_ps[:], func=ACT.Identity, accum_out=r_sum[:, a : a + 1]
+                )
+
+            neg_mean = tail.tile([P, ROW_TILES], F32, name="neg_mean")
+            nc.gpsimd.tensor_scalar(
+                out=neg_mean[:], in0=r_sum[:], scalar1=-1.0 / WIDTH, scalar2=0.0, op0=ALU.mult, op1=ALU.add
+            )
+            squares = tail.tile([P, ROW_TILES, WIDTH], BF16, name="squares")
+            dev_sq_sum = tail.tile([P, ROW_TILES], F32, name="dev_sq_sum")
+            for a in range(ROW_TILES):
+                nc.scalar.activation(
+                    out=squares[:, a, :],
+                    in_=r_sb[:, a, :],
+                    func=ACT.Square,
+                    bias=neg_mean[:, a : a + 1],
+                    scale=1.0,
+                    accum_out=dev_sq_sum[:, a : a + 1],
+                )
+            var_eps = tail.tile([P, ROW_TILES], F32, name="var_eps")
+            nc.gpsimd.tensor_scalar(
+                out=var_eps[:], in0=dev_sq_sum[:], scalar1=1.0 / WIDTH, scalar2=EPS, op0=ALU.mult, op1=ALU.add
+            )
+            rstd = tail.tile([P, ROW_TILES], F32, name="rstd")
+            nc.gpsimd.tensor_tensor(out=rstd[:], in0=var_eps[:], in1=neg_half[:], op=ALU.pow)
+
+            c_sb = tail.tile([P, ROW_TILES, WIDTH], F32, name="c_sb", bufs=4)
+            for a in range(ROW_TILES):
+                nc.vector.scalar_tensor_tensor(
+                    out=c_sb[:, a, :],
+                    in0=r_sb[:, a, :],
+                    scalar=neg_mean[:, a : a + 1],
+                    in1=clng_bc[:],
+                    op0=ALU.add,
+                    op1=ALU.mult,
+                )
+            for a in range(ROW_TILES):
+                nc.vector.scalar_tensor_tensor(
+                    out=c_sb[:, a, :],
+                    in0=c_sb[:, a, :],
+                    scalar=rstd[:, a : a + 1],
+                    in1=clnb_bc[:],
+                    op0=ALU.mult,
+                    op1=ALU.add,
+                )
+
+            c_max = max_over_variables(c_sb)
+            nc.vector.tensor_tensor(
+                out=by_variable(c_sb[:]), in0=by_variable(c_sb[:]), in1=over_variables(c_max[:]), op=ALU.subtract
+            )
+            nc.scalar.activation(out=c_sb[:], in_=c_sb[:], func=ACT.Exp)
+
+            e_sumT_ps = psum.tile([P, ROW_TILES, P], F32, name="e_sumT_ps", tag="e_sum_ps", bufs=1)
+            for a in range(ROW_TILES):
+                for j in range(FEAT_TILES):
+                    nc.tensor.matmul(
+                        out=e_sumT_ps[:, a, :],
+                        lhsT=c_sb[:, a, j * P : (j + 1) * P],
+                        rhs=ident_f32[:],
+                        start=(j == 0),
+                        stop=(j == FEAT_TILES - 1),
+                        is_transpose=True,
+                    )
+            e_sumT = tail.tile([P, ROW_TILES, P], F32, name="e_sumT", bufs=4)
+            nc.scalar.copy(out=e_sumT[:], in_=e_sumT_ps[:])
+            return c_sb, e_sumT
+
+        for first in range(0, N_CHUNKS, 2):
+            exponentials = [chunk_to_exponentials(first + i) for i in range(2)]
+            e_sum_inv = tail.tile([P, 2, ROW_TILES, D_FEAT], F32, name="e_sum_inv")
+            for i in range(2):
+                e_sumT = exponentials[i][1]
+                e_sum_ps = psum.tile([P, ROW_TILES, P], F32, name="e_sum_ps", tag="e_sum_ps", bufs=1)
+                for a in range(ROW_TILES):
+                    for moving, first_of_group in ((ident_f32, True), (swap_f32, False)):
+                        nc.tensor.matmul(
+                            out=e_sum_ps[:, a, :],
+                            lhsT=e_sumT[:, a, :],
+                            rhs=moving[:],
+                            start=first_of_group,
+                            stop=not first_of_group,
+                            is_transpose=True,
+                        )
+                nc.scalar.activation(out=e_sum_inv[:, i, :, :], in_=e_sum_ps[:, :, 0:D_FEAT], func=ACT.Ln)
+            nc.scalar.activation(out=e_sum_inv[:], in_=e_sum_inv[:], func=ACT.Exp, scale=-1.0)
+            for i in range(2):
+                c = first + i
+                out_sb = tail.tile([P, ROW_TILES, WIDTH], F32, name="out_sb")
+                nc.vector.tensor_tensor(
+                    out=by_variable(out_sb[:]),
+                    in0=by_variable(exponentials[i][0][:]),
+                    in1=over_variables(e_sum_inv[:, i, :, :]),
+                    op=ALU.mult,
+                )
+                nc.sync.dma_start(
+                    out=out[c * CHUNK : (c + 1) * CHUNK, :, :].rearrange("(p a) n d -> p a (n d)", a=ROW_TILES),
+                    in_=out_sb[:],
+                )

@@ -17,14 +17,17 @@ B = 4096
 WIDTH = 512
 N_VAR = 8
 D_FEAT = 64
-CHUNK = 512
-ROW_TILES = CHUNK // P
 FEAT_TILES = WIDTH // P
-N_CHUNKS = B // CHUNK
 EPS = 1e-5
 
 FLOPS = 3 * 2 * B * WIDTH * WIDTH
 
+SIZES = (2,) * 16
+GROUPS = (8, 6, 2)
+C_BUFS = 14
+MAXT = 2
+O_T, O_Q, O_M1, O_QE, O_M2, O_G, O_R = -5, -1, 2, 0.5, 2, 0.25, 1
+O_MEAN, O_SQ, O_N1, O_N2, O_MAX, O_SUB, O_EXP, O_S1, O_S2, O_INV, O_OUT, OUT_RATE = 0.1, 1.5, 1.75, 3.5, 4, 5, 7, 8.5, 9.5, 1, 0.5, 1
 
 def tile_variableselectionnetwork_pa_t_kernel(
     tc, h, x, cW1, cb1, cW4, cb4, cW5, cb5, clng, clnb, out
@@ -33,27 +36,42 @@ def tile_variableselectionnetwork_pa_t_kernel(
     with ExitStack() as ctx:
         consts = ctx.enter_context(tc.tile_pool(name="consts", bufs=1))
         setup = ctx.enter_context(tc.tile_pool(name="setup", bufs=1))
-        io = ctx.enter_context(tc.tile_pool(name="io", bufs=3))
-        work = ctx.enter_context(tc.tile_pool(name="work", bufs=2))
+        io = ctx.enter_context(tc.tile_pool(name="io", bufs=8))
+        work = ctx.enter_context(tc.tile_pool(name="work", bufs=3))
         gate = ctx.enter_context(tc.tile_pool(name="gate", bufs=2))
-        tail = ctx.enter_context(tc.tile_pool(name="tail", bufs=2))
+        tail = ctx.enter_context(tc.tile_pool(name="tail", bufs=3))
         psum = ctx.enter_context(tc.psum_pool(name="psum", bufs=2))
 
-        def load_chunk(c):
-            rows = slice(c * CHUNK, (c + 1) * CHUNK)
-            h_sb = io.tile([P, ROW_TILES, WIDTH], BF16, name="h_sb", tag="h_sb")
-            nc.sync.dma_start(out=h_sb[:], in_=h[rows, :].rearrange("(p a) k -> p a k", a=ROW_TILES))
-            x_sb = io.tile([P, ROW_TILES, WIDTH], BF16, name="x_sb", tag="x_sb")
-            nc.sync.dma_start(
-                out=x_sb[:], in_=x[rows, :, :].rearrange("(p a) n d -> p a (n d)", a=ROW_TILES)
-            )
-            return h_sb, x_sb
+        units = []
+        for nt in SIZES:
+            first = units[-1]["first"] + units[-1]["nt"] if units else 0
+            units.append({"first": first, "nt": nt, "rows": slice(first * P, (first + nt) * P)})
 
-        w1_raw = setup.tile([P, PACK, WIDTH], BF16, name="w1_raw")
-        nc.sync.dma_start(out=w1_raw[:], in_=cW1.rearrange("(p t) c -> p t c", t=PACK))
-        loaded = {0: load_chunk(0)}
+        def load_h(st):
+            st["h"] = io.tile([P, MAXT, WIDTH], BF16, name="h_sb")
+            nc.sync.dma_start(
+                out=st["h"][:, 0 : st["nt"], :], in_=h[st["rows"], :].rearrange("(p a) k -> p a k", a=st["nt"])
+            )
+
+        def load_x(st):
+            st["x"] = io.tile([P, MAXT, WIDTH], BF16, name="x_sb")
+            nc.sync.dma_start(
+                out=st["x"][:, 0 : st["nt"], :],
+                in_=x[st["rows"], :, :].rearrange("(p a) n d -> p a (n d)", a=st["nt"]),
+            )
+
+        def load_weight(w, name):
+            raw = setup.tile([P, PACK, WIDTH], BF16, name=name)
+            nc.sync.dma_start(out=raw[:], in_=w.rearrange("(p t) c -> p t c", t=PACK))
+            return raw
+
+        load_h(units[0])
+        w1_raw = load_weight(cW1, "w1_raw")
         cb1_raw = setup.tile([P, PACK], BF16, name="cb1_raw")
         nc.sync.dma_start(out=cb1_raw[:], in_=cb1.rearrange("(p t) -> p t", t=PACK))
+        load_h(units[1])
+        w5_raw = load_weight(cW5, "w5_raw")
+        w4_raw = load_weight(cW4, "w4_raw")
         bias_rows = setup.tile([P, P], BF16, name="bias_rows")
         nc.vector.memset(bias_rows[:], 0.0)
         for i, vec in enumerate((cb4, cb5)):
@@ -61,26 +79,26 @@ def tile_variableselectionnetwork_pa_t_kernel(
                 out=bias_rows[FEAT_TILES * i : FEAT_TILES * (i + 1), :],
                 in_=vec.rearrange("(t p) -> t p", p=P),
             )
-        w4_raw = setup.tile([P, PACK, WIDTH], BF16, name="w4_raw")
-        nc.sync.dma_start(out=w4_raw[:], in_=cW4.rearrange("(p t) c -> p t c", t=PACK))
-        w5_raw = setup.tile([P, PACK, WIDTH], BF16, name="w5_raw")
-        nc.sync.dma_start(out=w5_raw[:], in_=cW5.rearrange("(p t) c -> p t c", t=PACK))
+        load_h(units[2])
+        load_x(units[0])
         clng_bc = consts.tile([P, WIDTH], BF16, name="clng_bc")
-        nc.gpsimd.dma_start(out=clng_bc[:], in_=clng.partition_broadcast(P))
+        nc.sync.dma_start(out=clng_bc[:], in_=clng.partition_broadcast(P))
         clnb_bc = consts.tile([P, WIDTH], BF16, name="clnb_bc")
-        nc.gpsimd.dma_start(out=clnb_bc[:], in_=clnb.partition_broadcast(P))
+        nc.sync.dma_start(out=clnb_bc[:], in_=clnb.partition_broadcast(P))
+        for i in range(1, 6):
+            load_h(units[i + 2])
+            load_x(units[i])
 
         ident_f32 = consts.tile([P, P], F32, name="ident_f32")
         make_identity(nc, ident_f32[:])
         ident_bf16 = consts.tile([P, P], BF16, name="ident_bf16")
         make_identity(nc, ident_bf16[:])
-        swap_f32 = consts.tile([P, P], F32, name="swap_f32")
-        nc.vector.tensor_copy(out=swap_f32[:, 0:D_FEAT], in_=ident_f32[:, D_FEAT:P])
-        nc.vector.tensor_copy(out=swap_f32[:, D_FEAT:P], in_=ident_f32[:, 0:D_FEAT])
-        neg_half = consts.tile([P, ROW_TILES], F32, name="neg_half")
+        neg_half = consts.tile([P, MAXT], F32, name="neg_half")
         nc.vector.memset(neg_half[:], -0.5)
+        warm = consts.tile([P, 1], F32, name="warm")
+        nc.scalar.activation(out=warm[:], in_=neg_half[:, 0:1], func=ACT.Exp)
 
-        def quantise_weight(raw, copy, name, permute):
+        def regroup(raw, copy, name, permute):
             grouped = setup.tile([P, WIDTH, PACK], BF16, name=name + "_grouped", align_bytes=64)
             if permute:
                 copy(
@@ -92,6 +110,9 @@ def tile_variableselectionnetwork_pa_t_kernel(
                     out=grouped[:].rearrange("p (c i) t -> p c t i", i=4),
                     in_=raw[:].rearrange("p t (c i) -> p c t i", i=4),
                 )
+            return grouped
+
+        def quantise_weight(grouped, name):
             codes = consts.tile([P, WIDTH], U32, name=name + "_codes", align_bytes=64)
             scales = consts.tile([P, WIDTH], U8, name=name + "_scales", align_bytes=64)
             nc.vector.quantize_mx(
@@ -101,235 +122,352 @@ def tile_variableselectionnetwork_pa_t_kernel(
             )
             return codes, scales
 
-        w1_codes, w1_scales = quantise_weight(w1_raw, nc.vector.tensor_copy, "w1", True)
-        w4_codes, w4_scales = quantise_weight(w4_raw, nc.scalar.copy, "w4", False)
-        w5_codes, w5_scales = quantise_weight(w5_raw, nc.scalar.copy, "w5", False)
-
+        w1_grouped = regroup(w1_raw, nc.vector.tensor_copy, "w1", True)
+        w1_codes, w1_scales = quantise_weight(w1_grouped, "w1")
         cb1_cols = consts.tile([P, PACK], F32, name="cb1_cols")
         nc.vector.tensor_copy(out=cb1_cols[:], in_=cb1_raw[:])
-        bias_ps = psum.tile([P, P], BF16, name="bias_ps", tag="hT_ps", bufs=1)
-        nc.tensor.transpose(bias_ps[:], bias_rows[:], ident_bf16[:])
-        half_cb45_cols = consts.tile([P, 2 * FEAT_TILES], F32, name="half_cb45_cols")
-        nc.vector.tensor_scalar_mul(out=half_cb45_cols[:], in0=bias_ps[:, 0 : 2 * FEAT_TILES], scalar1=0.5)
-        half_cb4_cols = half_cb45_cols[:, 0:FEAT_TILES]
-        half_cb5_cols = half_cb45_cols[:, FEAT_TILES : 2 * FEAT_TILES]
-
-        def max_over_variables(src):
-            width = WIDTH
-            while width > D_FEAT:
-                width //= 2
-                dst = tail.tile([P, ROW_TILES, width], BF16, name="c_max_%d" % width)
-                nc.vector.tensor_tensor(
-                    out=dst[:], in0=src[:, :, 0:width], in1=src[:, :, width : 2 * width], op=ALU.max
-                )
-                src = dst
-            return src
-
         def over_variables(per_feature):
-            return per_feature.unsqueeze(2).to_broadcast([P, ROW_TILES, N_VAR, D_FEAT])
+            return per_feature.unsqueeze(1).to_broadcast([P, N_VAR, D_FEAT])
 
         def by_variable(tile_ap):
-            return tile_ap.rearrange("p a (n d) -> p a n d", n=N_VAR)
+            return tile_ap.rearrange("p (n d) -> p n d", n=N_VAR)
 
-        def chunk_to_exponentials(c):
-            if c + 1 < N_CHUNKS:
-                loaded[c + 1] = load_chunk(c + 1)
-            h_sb, x_sb = loaded[c]
-
-            h_grouped = work.tile([P, CHUNK * PACK], BF16, name="h_grouped", align_bytes=64)
-            h_grouped_words = h_grouped[:].bitcast(F32).rearrange(
-                "q (a b u) -> q a b u", a=ROW_TILES, u=2
+        def transpose_h(st, a):
+            nt = st["nt"]
+            if a == 0:
+                st["h_grouped"] = work.tile([P, MAXT * P * PACK], BF16, name="h_grouped", align_bytes=64)
+            n = min(2, nt)
+            hT_ps = psum.tile([P, 2, 2, P], F32, name="hT_ps", tag="hT_ps", bufs=1)
+            for i in range(n):
+                h_words = st["h"][:, a + i, :].bitcast(F32)
+                for w in range(2):
+                    nc.tensor.transpose(hT_ps[:, i, w, :], h_words[:, w : 2 * P : 2], ident_f32[:])
+            nc.scalar.copy(
+                out=st["h_grouped"][:].bitcast(F32).rearrange("q (a b w) -> q a b w", a=MAXT, w=2)[:, a : a + n, :, :],
+                in_=hT_ps[:, 0:n, :, :].rearrange("q a w b -> q a b w"),
             )
-            for pair in range(ROW_TILES // 2):
-                hT_ps = psum.tile([P, 2, 2, P], F32, name="hT_ps", tag="hT_ps", bufs=1)
-                for a in range(2):
-                    h_words = h_sb[:, 2 * pair + a, :].bitcast(F32)
-                    for u in range(2):
-                        nc.tensor.transpose(
-                            hT_ps[:, a, u, :], h_words[:, u : 2 * P : 2], ident_f32[:]
-                        )
-                nc.scalar.copy(
-                    out=h_grouped_words[:, 2 * pair : 2 * pair + 2, :, :],
-                    in_=hT_ps[:].rearrange("q a u b -> q a b u"),
-                )
-            h_codes = work.tile([P, CHUNK], U32, name="h_codes", align_bytes=64)
-            h_scales = work.tile([P, CHUNK], U8, name="h_scales", align_bytes=64)
-            nc.vector.quantize_mx(out=h_codes[:].bitcast(FP8X4), scales=h_scales[:], in_=h_grouped[:])
 
-            e1_grouped = work.tile([P, CHUNK, PACK], BF16, name="e1_grouped", align_bytes=64)
-            for a in range(ROW_TILES):
-                cols = slice(a * P, (a + 1) * P)
-                e1_ps = psum.tile([P, PACK, P], F32, name="e1_ps", tag="e1_ps")
-                for t in range(PACK):
-                    feats = slice(t * P, (t + 1) * P)
-                    nc.tensor.matmul_mx(
-                        out=e1_ps[:, t, :],
-                        lhsT=w1_codes[:, feats].bitcast(FP8X4),
-                        lhsT_scale=w1_scales[:, feats],
-                        rhs=h_codes[:, cols].bitcast(FP8X4),
-                        rhs_scale=h_scales[:, cols],
-                        start=True,
-                        stop=True,
-                    )
-                nc.vector.tensor_tensor(
-                    out=e1_grouped[:, cols, :],
-                    in0=e1_ps[:].rearrange("p t b -> p b t"),
-                    in1=cb1_cols[:].unsqueeze(1).to_broadcast([P, P, PACK]),
-                    op=ALU.add,
-                )
-            e1_codes = work.tile([P, CHUNK], U32, name="e1_codes", align_bytes=64)
-            e1_scales = work.tile([P, CHUNK], U8, name="e1_scales", align_bytes=64)
+        def quantise_h(st):
+            rows = st["nt"] * P
+            st["h_codes"] = work.tile([P, MAXT * P], U32, name="h_codes", align_bytes=64)
+            st["h_scales"] = work.tile([P, MAXT * P], U8, name="h_scales", align_bytes=64)
             nc.vector.quantize_mx(
-                out=e1_codes[:].bitcast(FP8X4),
-                scales=e1_scales[:],
-                in_=e1_grouped[:].rearrange("p b t -> p (b t)"),
+                out=st["h_codes"][:, 0:rows].bitcast(FP8X4),
+                scales=st["h_scales"][:, 0:rows],
+                in_=st["h_grouped"][:, 0 : rows * PACK],
             )
 
-            gT = gate.tile([P, FEAT_TILES, CHUNK], F32, name="gT")
-            for j2 in range(0, FEAT_TILES, 2):
-                tanh_sb = gate.tile([P, 2, CHUNK], F32, name="tanh_sb")
-                half_lin_sb = gate.tile([P, 2, CHUNK], F32, name="half_lin_sb")
-                for i in range(2):
-                    j = j2 + i
-                    feats = slice(j * P, (j + 1) * P)
-                    u4_ps = psum.tile([P, CHUNK], F32, name="u4_ps", tag="u_ps")
-                    u5_ps = psum.tile([P, CHUNK], F32, name="u5_ps", tag="u_ps")
-                    for u_ps, codes, scales in ((u4_ps, w4_codes, w4_scales), (u5_ps, w5_codes, w5_scales)):
-                        nc.tensor.matmul_mx(
-                            out=u_ps[:],
-                            lhsT=codes[:, feats].bitcast(FP8X4),
-                            lhsT_scale=scales[:, feats],
-                            rhs=e1_codes[:].bitcast(FP8X4),
-                            rhs_scale=e1_scales[:],
-                            start=True,
-                            stop=True,
-                        )
-                    nc.scalar.activation(
-                        out=tanh_sb[:, i, :], in_=u4_ps[:], func=ACT.Tanh, bias=half_cb4_cols[:, j : j + 1], scale=0.5
-                    )
-                    nc.scalar.activation(
-                        out=half_lin_sb[:, i, :],
-                        in_=u5_ps[:],
-                        func=ACT.Identity,
-                        bias=half_cb5_cols[:, j : j + 1],
-                        scale=0.5,
-                    )
-                nc.vector.scalar_tensor_tensor(
-                    out=gT[:, j2 : j2 + 2, :], in0=tanh_sb[:], scalar=1.0, in1=half_lin_sb[:], op0=ALU.add, op1=ALU.mult
+        def first_product(st, a):
+            if a == 0:
+                st["e1_grouped"] = work.tile([P, MAXT * P, PACK], BF16, name="e1_grouped", align_bytes=64)
+            cols = slice(a * P, (a + 1) * P)
+            e1_ps = psum.tile([P, PACK, P], F32, name="e1_ps", tag="e1_ps", bufs=2)
+            for t in range(PACK):
+                feats = slice(t * P, (t + 1) * P)
+                nc.tensor.matmul_mx(
+                    out=e1_ps[:, t, :],
+                    lhsT=w1_codes[:, feats].bitcast(FP8X4),
+                    lhsT_scale=w1_scales[:, feats],
+                    rhs=st["h_codes"][:, cols].bitcast(FP8X4),
+                    rhs_scale=st["h_scales"][:, cols],
+                    start=True,
+                    stop=True,
                 )
-
-            r_sb = tail.tile([P, ROW_TILES, WIDTH], F32, name="r_sb")
-            r_sum = tail.tile([P, ROW_TILES], F32, name="r_sum")
-            for a in range(ROW_TILES):
-                r_ps = psum.tile([P, WIDTH], F32, name="r_ps", tag="r_ps")
-                for j in range(FEAT_TILES):
-                    feats = slice(j * P, (j + 1) * P)
-                    nc.tensor.matmul(
-                        out=r_ps[:, feats], lhsT=ident_bf16[:], rhs=x_sb[:, a, feats], start=True, stop=False
-                    )
-                    nc.tensor.matmul(
-                        out=r_ps[:, feats],
-                        lhsT=gT[:, j, a * P : (a + 1) * P],
-                        rhs=ident_f32[:],
-                        start=False,
-                        stop=True,
-                        is_transpose=True,
-                    )
-                nc.scalar.activation(
-                    out=r_sb[:, a, :], in_=r_ps[:], func=ACT.Identity, accum_out=r_sum[:, a : a + 1]
-                )
-
-            neg_mean = tail.tile([P, ROW_TILES], F32, name="neg_mean")
-            nc.gpsimd.tensor_scalar(
-                out=neg_mean[:], in0=r_sum[:], scalar1=-1.0 / WIDTH, scalar2=0.0, op0=ALU.mult, op1=ALU.add
-            )
-            squares = tail.tile([P, ROW_TILES, WIDTH], BF16, name="squares")
-            dev_sq_sum = tail.tile([P, ROW_TILES], F32, name="dev_sq_sum")
-            for a in range(ROW_TILES):
-                nc.scalar.activation(
-                    out=squares[:, a, :],
-                    in_=r_sb[:, a, :],
-                    func=ACT.Square,
-                    bias=neg_mean[:, a : a + 1],
-                    scale=1.0,
-                    accum_out=dev_sq_sum[:, a : a + 1],
-                )
-            var_eps = tail.tile([P, ROW_TILES], F32, name="var_eps")
-            nc.gpsimd.tensor_scalar(
-                out=var_eps[:], in0=dev_sq_sum[:], scalar1=1.0 / WIDTH, scalar2=EPS, op0=ALU.mult, op1=ALU.add
-            )
-            rstd = tail.tile([P, ROW_TILES], F32, name="rstd")
-            nc.gpsimd.tensor_tensor(out=rstd[:], in0=var_eps[:], in1=neg_half[:], op=ALU.pow)
-
-            c_sb = tail.tile([P, ROW_TILES, WIDTH], F32, name="c_sb", bufs=4)
-            for a in range(ROW_TILES):
-                nc.vector.scalar_tensor_tensor(
-                    out=c_sb[:, a, :],
-                    in0=r_sb[:, a, :],
-                    scalar=neg_mean[:, a : a + 1],
-                    in1=clng_bc[:],
-                    op0=ALU.add,
-                    op1=ALU.mult,
-                )
-            for a in range(ROW_TILES):
-                nc.vector.scalar_tensor_tensor(
-                    out=c_sb[:, a, :],
-                    in0=c_sb[:, a, :],
-                    scalar=rstd[:, a : a + 1],
-                    in1=clnb_bc[:],
-                    op0=ALU.mult,
-                    op1=ALU.add,
-                )
-
-            c_max = max_over_variables(c_sb)
             nc.vector.tensor_tensor(
-                out=by_variable(c_sb[:]), in0=by_variable(c_sb[:]), in1=over_variables(c_max[:]), op=ALU.subtract
+                out=st["e1_grouped"][:, cols, :],
+                in0=e1_ps[:].rearrange("p t b -> p b t"),
+                in1=cb1_cols[:].unsqueeze(1).to_broadcast([P, P, PACK]),
+                op=ALU.add,
             )
-            nc.scalar.activation(out=c_sb[:], in_=c_sb[:], func=ACT.Exp)
 
-            e_sumT_ps = psum.tile([P, ROW_TILES, P], F32, name="e_sumT_ps", tag="e_sum_ps", bufs=1)
-            for a in range(ROW_TILES):
+        def quantise_e1(st):
+            rows = st["nt"] * P
+            st["e1_codes"] = work.tile([P, MAXT * P], U32, name="e1_codes", align_bytes=64)
+            st["e1_scales"] = work.tile([P, MAXT * P], U8, name="e1_scales", align_bytes=64)
+            nc.vector.quantize_mx(
+                out=st["e1_codes"][:, 0:rows].bitcast(FP8X4),
+                scales=st["e1_scales"][:, 0:rows],
+                in_=st["e1_grouped"][:, 0:rows, :].rearrange("p b t -> p (b t)"),
+            )
+
+        def second_product(st, j):
+            rows = st["nt"] * P
+            if j == 0:
+                st["tanh"] = gate.tile([P, FEAT_TILES, MAXT * P], F32, name="tanh_sb")
+                st["lin"] = gate.tile([P, FEAT_TILES, MAXT * P], F32, name="half_lin_sb")
+            feats = slice(j * P, (j + 1) * P)
+            for dst, codes, scales, func, bias in (
+                ("tanh", w4_codes, w4_scales, ACT.Tanh, half_cb4_cols),
+                ("lin", w5_codes, w5_scales, ACT.Identity, half_cb5_cols),
+            ):
+                u_ps = psum.tile([P, MAXT * P], F32, name="u_ps", tag="u_ps", bufs=2)
+                nc.tensor.matmul_mx(
+                    out=u_ps[:, 0:rows],
+                    lhsT=codes[:, feats].bitcast(FP8X4),
+                    lhsT_scale=scales[:, feats],
+                    rhs=st["e1_codes"][:, 0:rows].bitcast(FP8X4),
+                    rhs_scale=st["e1_scales"][:, 0:rows],
+                    start=True,
+                    stop=True,
+                )
+                nc.scalar.activation(
+                    out=st[dst][:, j, 0:rows], in_=u_ps[:, 0:rows], func=func, bias=bias[:, j : j + 1], scale=0.5
+                )
+
+        def gate_product(st, j2):
+            rows = st["nt"] * P
+            if j2 == 0:
+                st["gT"] = gate.tile([P, FEAT_TILES, MAXT * P], F32, name="gT")
+            nc.vector.scalar_tensor_tensor(
+                out=st["gT"][:, j2 : j2 + 2, 0:rows],
+                in0=st["tanh"][:, j2 : j2 + 2, 0:rows],
+                scalar=1.0,
+                in1=st["lin"][:, j2 : j2 + 2, 0:rows],
+                op0=ALU.add,
+                op1=ALU.mult,
+            )
+
+        def residual(st, a):
+            if a == 0:
+                st["r"] = tail.tile([P, MAXT, WIDTH], F32, name="r_sb")
+                st["r_sum"] = tail.tile([P, MAXT], F32, name="r_sum")
+                st["neg_mean"] = tail.tile([P, MAXT], F32, name="neg_mean")
+            r_ps = psum.tile([P, WIDTH], F32, name="r_ps", tag="r_ps", bufs=2)
+            nc.tensor.matmul(out=r_ps[:], lhsT=ident_bf16[:], rhs=st["x"][:, a, :], start=True, stop=False)
+            for j in range(FEAT_TILES):
+                nc.tensor.matmul(
+                    out=r_ps[:, j * P : (j + 1) * P],
+                    lhsT=st["gT"][:, j, a * P : (a + 1) * P],
+                    rhs=ident_f32[:],
+                    start=False,
+                    stop=(j == FEAT_TILES - 1),
+                    is_transpose=True,
+                )
+            nc.scalar.activation(
+                out=st["r"][:, a, :], in_=r_ps[:], func=ACT.Identity, accum_out=st["r_sum"][:, a : a + 1]
+            )
+
+        def mean(st, a, n):
+            nc.gpsimd.tensor_scalar(
+                out=st["neg_mean"][:, a : a + n],
+                in0=st["r_sum"][:, a : a + n],
+                scalar1=-1.0 / WIDTH,
+                scalar2=0.0,
+                op0=ALU.mult,
+                op1=ALU.add,
+            )
+
+        def squares(st, a):
+            if a == 0:
+                st["dev"] = tail.tile([P, MAXT], F32, name="dev_sq_sum")
+                st["var"] = tail.tile([P, MAXT], F32, name="var_eps")
+                st["rstd"] = tail.tile([P, MAXT], F32, name="rstd")
+            sq = tail.tile([P, WIDTH], BF16, name="squares", bufs=1)
+            nc.scalar.activation(
+                out=sq[:],
+                in_=st["r"][:, a, :],
+                func=ACT.Square,
+                bias=st["neg_mean"][:, a : a + 1],
+                scale=1.0,
+                accum_out=st["dev"][:, a : a + 1],
+            )
+
+        def reciprocal_std(st, a, n):
+            nc.gpsimd.tensor_scalar(
+                out=st["var"][:, a : a + n],
+                in0=st["dev"][:, a : a + n],
+                scalar1=1.0 / WIDTH,
+                scalar2=EPS,
+                op0=ALU.mult,
+                op1=ALU.add,
+            )
+            nc.gpsimd.tensor_tensor(
+                out=st["rstd"][:, a : a + n], in0=st["var"][:, a : a + n], in1=neg_half[:, 0:n], op=ALU.pow
+            )
+
+        def normalise_1(st, a):
+            if a == 0:
+                st["c"] = tail.tile([P, MAXT, WIDTH], F32, name="c_sb", bufs=C_BUFS)
+            nc.vector.scalar_tensor_tensor(
+                out=st["c"][:, a, :],
+                in0=st["r"][:, a, :],
+                scalar=st["neg_mean"][:, a : a + 1],
+                in1=clng_bc[:],
+                op0=ALU.add,
+                op1=ALU.mult,
+            )
+
+        def normalise_2(st, a):
+            nc.vector.scalar_tensor_tensor(
+                out=st["c"][:, a, :],
+                in0=st["c"][:, a, :],
+                scalar=st["rstd"][:, a : a + 1],
+                in1=clnb_bc[:],
+                op0=ALU.mult,
+                op1=ALU.add,
+            )
+
+        def maximum(st, a, n, level):
+            width = WIDTH >> (level + 1)
+            src = st["max%d" % (level - 1)][:, a : a + n, :] if level else st["c"][:, a : a + n, :]
+            if a == 0:
+                st["max%d" % level] = tail.tile([P, MAXT, width], BF16, name="c_max_%d" % width)
+            nc.vector.tensor_tensor(
+                out=st["max%d" % level][:, a : a + n, :],
+                in0=src[:, :, 0:width],
+                in1=src[:, :, width : 2 * width],
+                op=ALU.max,
+            )
+
+        def subtract_max(st, a):
+            nc.vector.tensor_tensor(
+                out=by_variable(st["c"][:, a, :]),
+                in0=by_variable(st["c"][:, a, :]),
+                in1=over_variables(st["max2"][:, a, :]),
+                op=ALU.subtract,
+            )
+
+        def exponentials(st, a, n):
+            nc.scalar.activation(out=st["c"][:, a : a + n, :], in_=st["c"][:, a : a + n, :], func=ACT.Exp)
+
+        def sums_1(st, a, n):
+            if a == 0:
+                st["e_sumT"] = tail.tile([P, MAXT, P], F32, name="e_sumT", bufs=2)
+            e_sumT_ps = psum.tile([P, MAXT, P], F32, name="e_sumT_ps", tag="e_sum_ps", bufs=1)
+            for i in range(n):
                 for j in range(FEAT_TILES):
                     nc.tensor.matmul(
-                        out=e_sumT_ps[:, a, :],
-                        lhsT=c_sb[:, a, j * P : (j + 1) * P],
+                        out=e_sumT_ps[:, i, :],
+                        lhsT=st["c"][:, a + i, j * P : (j + 1) * P],
                         rhs=ident_f32[:],
                         start=(j == 0),
                         stop=(j == FEAT_TILES - 1),
                         is_transpose=True,
                     )
-            e_sumT = tail.tile([P, ROW_TILES, P], F32, name="e_sumT", bufs=4)
-            nc.scalar.copy(out=e_sumT[:], in_=e_sumT_ps[:])
-            return c_sb, e_sumT
+            nc.scalar.copy(out=st["e_sumT"][:, a : a + n, :], in_=e_sumT_ps[:, 0:n, :])
 
-        for first in range(0, N_CHUNKS, 2):
-            exponentials = [chunk_to_exponentials(first + i) for i in range(2)]
-            e_sum_inv = tail.tile([P, 2, ROW_TILES, D_FEAT], F32, name="e_sum_inv")
-            for i in range(2):
-                e_sumT = exponentials[i][1]
-                e_sum_ps = psum.tile([P, ROW_TILES, P], F32, name="e_sum_ps", tag="e_sum_ps", bufs=1)
-                for a in range(ROW_TILES):
-                    for moving, first_of_group in ((ident_f32, True), (swap_f32, False)):
-                        nc.tensor.matmul(
-                            out=e_sum_ps[:, a, :],
-                            lhsT=e_sumT[:, a, :],
-                            rhs=moving[:],
-                            start=first_of_group,
-                            stop=not first_of_group,
-                            is_transpose=True,
-                        )
-                nc.scalar.activation(out=e_sum_inv[:, i, :, :], in_=e_sum_ps[:, :, 0:D_FEAT], func=ACT.Ln)
-            nc.scalar.activation(out=e_sum_inv[:], in_=e_sum_inv[:], func=ACT.Exp, scale=-1.0)
-            for i in range(2):
-                c = first + i
-                out_sb = tail.tile([P, ROW_TILES, WIDTH], F32, name="out_sb")
-                nc.vector.tensor_tensor(
-                    out=by_variable(out_sb[:]),
-                    in0=by_variable(exponentials[i][0][:]),
-                    in1=over_variables(e_sum_inv[:, i, :, :]),
-                    op=ALU.mult,
-                )
+        def sums_2(st, a, n):
+            if a == 0:
+                st["e_sum"] = tail.tile([P, MAXT, D_FEAT], F32, name="e_sum", bufs=C_BUFS)
+            e_sum_ps = psum.tile([P, MAXT, P], F32, name="e_sum_ps", tag="e_sum_ps", bufs=1)
+            for i in range(n):
+                for moving, first_of_group in ((ident_f32, True), (swap_f32, False)):
+                    nc.tensor.matmul(
+                        out=e_sum_ps[:, i, :],
+                        lhsT=st["e_sumT"][:, a + i, :],
+                        rhs=moving[:],
+                        start=first_of_group,
+                        stop=not first_of_group,
+                        is_transpose=True,
+                    )
+            nc.scalar.copy(out=st["e_sum"][:, a : a + n, :], in_=e_sum_ps[:, 0:n, 0:D_FEAT])
+
+        def invert(group):
+            for st in group:
+                nt = st["nt"]
+                nc.scalar.activation(out=st["e_sum"][:, 0:nt, :], in_=st["e_sum"][:, 0:nt, :], func=ACT.Ln)
+            for st in group:
+                nt = st["nt"]
+                nc.scalar.activation(out=st["e_sum"][:, 0:nt, :], in_=st["e_sum"][:, 0:nt, :], func=ACT.Exp, scale=-1.0)
+
+        def output(st, a):
+            if a == 0:
+                st["out"] = tail.tile([P, MAXT, WIDTH], F32, name="out_sb", bufs=5)
+            nc.vector.tensor_tensor(
+                out=by_variable(st["out"][:, a, :]),
+                in0=by_variable(st["c"][:, a, :]),
+                in1=over_variables(st["e_sum"][:, a, :]),
+                op=ALU.mult,
+            )
+            if a == st["nt"] - 1:
                 nc.sync.dma_start(
-                    out=out[c * CHUNK : (c + 1) * CHUNK, :, :].rearrange("(p a) n d -> p a (n d)", a=ROW_TILES),
-                    in_=out_sb[:],
+                    out=out[st["rows"], :, :].rearrange("(p a) n d -> p a (n d)", a=st["nt"]),
+                    in_=st["out"][:, 0 : st["nt"], :],
                 )
+
+        transpose_h(units[0], 0)
+        quantise_h(units[0])
+        transpose_h(units[1], 0)
+        w5_grouped = regroup(w5_raw, nc.vector.tensor_copy, "w5", False)
+        w4_grouped = regroup(w4_raw, nc.scalar.copy, "w4", False)
+        swap_f32 = consts.tile([P, P], F32, name="swap_f32")
+        nc.vector.tensor_copy(out=swap_f32[:, 0:D_FEAT], in_=ident_f32[:, D_FEAT:P])
+        nc.vector.tensor_copy(out=swap_f32[:, D_FEAT:P], in_=ident_f32[:, 0:D_FEAT])
+        for a in range(MAXT):
+            first_product(units[0], a)
+        quantise_e1(units[0])
+        w4_codes, w4_scales = quantise_weight(w4_grouped, "w4")
+        w5_codes, w5_scales = quantise_weight(w5_grouped, "w5")
+        bias_ps = psum.tile([P, P], BF16, name="bias_ps", tag="e_sum_ps", bufs=1)
+        nc.tensor.transpose(bias_ps[:], bias_rows[:], ident_bf16[:])
+        half_cb45_cols = consts.tile([P, 2 * FEAT_TILES], F32, name="half_cb45_cols")
+        nc.vector.tensor_scalar_mul(out=half_cb45_cols[:], in0=bias_ps[:, 0 : 2 * FEAT_TILES], scalar1=0.5)
+        half_cb4_cols = half_cb45_cols[:, 0:FEAT_TILES]
+        half_cb5_cols = half_cb45_cols[:, FEAT_TILES : 2 * FEAT_TILES]
+        quantise_h(units[1])
+
+        steps = []
+
+        def at(when, what, *args):
+            steps.append((when, len(steps), what, args))
+
+        group_of = []
+        for i, n in enumerate(GROUPS):
+            group_of += [i] * n
+        for i, st in enumerate(units):
+            nt, f = st["nt"], st["first"]
+            pair = min(2, nt)
+            if i > 7:
+                at(f - 10, load_h, st)
+            if i > 5:
+                at(f - 8, load_x, st)
+            t0 = f + O_T
+            if i > 1:
+                for a in range(0, nt, pair):
+                    at(t0 + a, transpose_h, st, a)
+            t1 = t0 + nt + O_Q
+            if i > 1:
+                at(t1, quantise_h, st)
+            t1 += O_M1
+            if i > 0:
+                for a in range(nt):
+                    at(t1 + a, first_product, st, a)
+            t2 = t1 + nt + O_QE
+            if i > 0:
+                at(t2, quantise_e1, st)
+            t2 += O_M2
+            for j in range(FEAT_TILES):
+                at(t2 + j * nt / FEAT_TILES, second_product, st, j)
+            for j2 in (0, 2):
+                at(t2 + (j2 + 2) * nt / FEAT_TILES + O_G, gate_product, st, j2)
+            t3 = t2 + nt + O_R
+            for a in range(nt):
+                at(t3 + a, residual, st, a)
+                if a % pair == pair - 1:
+                    at(t3 + a + O_MEAN, mean, st, a - pair + 1, pair)
+                at(t3 + a + O_SQ, squares, st, a)
+                at(t3 + a + O_N1, normalise_1, st, a)
+                if a % pair == pair - 1:
+                    at(t3 + a + O_SQ, reciprocal_std, st, a - pair + 1, pair)
+                at(t3 + a + O_N2, normalise_2, st, a)
+                if a % pair == pair - 1:
+                    b = a - pair + 1
+                    for level in range(3):
+                        at(t3 + a + O_MAX + 0.3 * level, maximum, st, b, pair, level)
+                    for k in range(b, a + 1):
+                        at(t3 + k + 1 + O_SUB, subtract_max, st, k)
+                    at(t3 + a + O_EXP, exponentials, st, b, pair)
+                    at(t3 + a + O_S1, sums_1, st, b, pair)
+                    at(t3 + a + O_S2, sums_2, st, b, pair)
+            if i + 1 == len(units) or group_of[i + 1] != group_of[i]:
+                group = [units[k] for k in range(len(units)) if group_of[k] == group_of[i]]
+                t5 = t3 + nt - 1 + O_S2 + O_INV
+                at(t5, invert, group)
+                n = 0
+                for g in group:
+                    for a in range(g["nt"]):
+                        n += 1
+                        at(t5 + O_OUT + n * OUT_RATE, output, g, a)
+        with tc.manual_schedule():
+            for when, n, what, args in sorted(steps, key=lambda s: (s[0], s[1])):
+                what(*args)

@@ -196,13 +196,10 @@ def tile_variableselectionnetwork_pa_t_kernel(
                 st["tanh"] = gate.tile([P, FEAT_TILES, MAXT * P], F32, name="tanh_sb")
                 st["lin"] = gate.tile([P, FEAT_TILES, MAXT * P], F32, name="half_lin_sb")
             feats = slice(j * P, (j + 1) * P)
-            for dst, codes, scales, func, bias in (
-                ("tanh", w4_codes, w4_scales, ACT.Tanh, half_cb4_cols),
-                ("lin", w5_codes, w5_scales, ACT.Identity, half_cb5_cols),
-            ):
-                u_ps = psum.tile([P, MAXT * P], F32, name="u_ps", tag="u_ps", bufs=2)
+            u_ps = psum.tile([P, 2, MAXT * P], F32, name="u_ps", tag="u_ps", bufs=2)
+            for i, codes, scales in ((0, w4_codes, w4_scales), (1, w5_codes, w5_scales)):
                 nc.tensor.matmul_mx(
-                    out=u_ps[:, 0:rows],
+                    out=u_ps[:, i, 0:rows],
                     lhsT=codes[:, feats].bitcast(FP8X4),
                     lhsT_scale=scales[:, feats],
                     rhs=st["e1_codes"][:, 0:rows].bitcast(FP8X4),
@@ -210,8 +207,9 @@ def tile_variableselectionnetwork_pa_t_kernel(
                     start=True,
                     stop=True,
                 )
+            for i, dst, func, bias in ((0, "tanh", ACT.Tanh, half_cb4_cols), (1, "lin", ACT.Identity, half_cb5_cols)):
                 nc.scalar.activation(
-                    out=st[dst][:, j, 0:rows], in_=u_ps[:, 0:rows], func=func, bias=bias[:, j : j + 1], scale=0.5
+                    out=st[dst][:, j, 0:rows], in_=u_ps[:, i, 0:rows], func=func, bias=bias[:, j : j + 1], scale=0.5
                 )
 
         def gate_product(st, j2):

@@ -25,9 +25,10 @@ FLOPS = 3 * 2 * B * WIDTH * WIDTH
 SIZES = (2,) * 16
 GROUPS = (8, 6, 2)
 C_BUFS = 14
+MAX_GROUP = 16
 MAXT = 2
 O_T, O_Q, O_M1, O_QE, O_M2, O_G, O_R = -5, -1, 2, 0.5, 2, 0.25, 1
-O_MEAN, O_SQ, O_N1, O_N2, O_MAX, O_SUB, O_EXP, O_S1, O_S2, O_INV, O_OUT, OUT_RATE = 0.1, 1.5, 1.75, 3.5, 4, 5, 7, 8.5, 9.5, 1, 0.5, 1
+O_MEAN, O_SQ, O_N1, O_N2, O_MAX, O_SUB, O_EXP, O_S1, O_S2, O_INV, O_OUT, OUT_RATE = 0.1, 0.6, 0.7, 3.5, 4, 5, 7, 8.5, 9.5, 1, 0.5, 1
 
 def tile_variableselectionnetwork_pa_t_kernel(
     tc, h, x, cW1, cb1, cW4, cb4, cW5, cb5, clng, clnb, out
@@ -127,10 +128,10 @@ def tile_variableselectionnetwork_pa_t_kernel(
         cb1_cols = consts.tile([P, PACK], F32, name="cb1_cols")
         nc.vector.tensor_copy(out=cb1_cols[:], in_=cb1_raw[:])
         def over_variables(per_feature):
-            return per_feature.unsqueeze(1).to_broadcast([P, N_VAR, D_FEAT])
+            return per_feature.unsqueeze(2).to_broadcast([P, per_feature.shape[1], N_VAR, D_FEAT])
 
         def by_variable(tile_ap):
-            return tile_ap.rearrange("p (n d) -> p n d", n=N_VAR)
+            return tile_ap.rearrange("p a (n d) -> p a n d", n=N_VAR)
 
         def transpose_h(st, a):
             nt = st["nt"]
@@ -227,10 +228,10 @@ def tile_variableselectionnetwork_pa_t_kernel(
 
         def residual(st, a):
             if a == 0:
-                st["r"] = tail.tile([P, MAXT, WIDTH], F32, name="r_sb")
-                st["r_sum"] = tail.tile([P, MAXT], F32, name="r_sum")
+                st["r"] = []
                 st["neg_mean"] = tail.tile([P, MAXT], F32, name="neg_mean")
             r_ps = psum.tile([P, WIDTH], F32, name="r_ps", tag="r_ps", bufs=2)
+            st["r"].append(r_ps)
             nc.tensor.matmul(out=r_ps[:], lhsT=ident_bf16[:], rhs=st["x"][:, a, :], start=True, stop=False)
             for j in range(FEAT_TILES):
                 nc.tensor.matmul(
@@ -241,18 +242,15 @@ def tile_variableselectionnetwork_pa_t_kernel(
                     stop=(j == FEAT_TILES - 1),
                     is_transpose=True,
                 )
-            nc.scalar.activation(
-                out=st["r"][:, a, :], in_=r_ps[:], func=ACT.Identity, accum_out=st["r_sum"][:, a : a + 1]
-            )
 
-        def mean(st, a, n):
-            nc.gpsimd.tensor_scalar(
-                out=st["neg_mean"][:, a : a + n],
-                in0=st["r_sum"][:, a : a + n],
-                scalar1=-1.0 / WIDTH,
-                scalar2=0.0,
-                op0=ALU.mult,
-                op1=ALU.add,
+        def mean(st, a):
+            unused = tail.tile([P, WIDTH], BF16, name="unused", bufs=1)
+            nc.scalar.activation(
+                out=unused[:],
+                in_=st["r"][a][:],
+                func=ACT.Identity,
+                scale=-1.0 / WIDTH,
+                accum_out=st["neg_mean"][:, a : a + 1],
             )
 
         def squares(st, a):
@@ -260,10 +258,10 @@ def tile_variableselectionnetwork_pa_t_kernel(
                 st["dev"] = tail.tile([P, MAXT], F32, name="dev_sq_sum")
                 st["var"] = tail.tile([P, MAXT], F32, name="var_eps")
                 st["rstd"] = tail.tile([P, MAXT], F32, name="rstd")
-            sq = tail.tile([P, WIDTH], BF16, name="squares", bufs=1)
+            unused = tail.tile([P, WIDTH], BF16, name="unused", bufs=1)
             nc.scalar.activation(
-                out=sq[:],
-                in_=st["r"][:, a, :],
+                out=unused[:],
+                in_=st["r"][a][:],
                 func=ACT.Square,
                 bias=st["neg_mean"][:, a : a + 1],
                 scale=1.0,
@@ -288,7 +286,7 @@ def tile_variableselectionnetwork_pa_t_kernel(
                 st["c"] = tail.tile([P, MAXT, WIDTH], F32, name="c_sb", bufs=C_BUFS)
             nc.vector.scalar_tensor_tensor(
                 out=st["c"][:, a, :],
-                in0=st["r"][:, a, :],
+                in0=st["r"][a][:],
                 scalar=st["neg_mean"][:, a : a + 1],
                 in1=clng_bc[:],
                 op0=ALU.add,
@@ -317,11 +315,11 @@ def tile_variableselectionnetwork_pa_t_kernel(
                 op=ALU.max,
             )
 
-        def subtract_max(st, a):
+        def subtract_max(st, a, n):
             nc.vector.tensor_tensor(
-                out=by_variable(st["c"][:, a, :]),
-                in0=by_variable(st["c"][:, a, :]),
-                in1=over_variables(st["max2"][:, a, :]),
+                out=by_variable(st["c"][:, a : a + n, :]),
+                in0=by_variable(st["c"][:, a : a + n, :]),
+                in1=over_variables(st["max2"][:, a : a + n, :]),
                 op=ALU.subtract,
             )
 
@@ -345,8 +343,11 @@ def tile_variableselectionnetwork_pa_t_kernel(
             nc.scalar.copy(out=st["e_sumT"][:, a : a + n, :], in_=e_sumT_ps[:, 0:n, :])
 
         def sums_2(st, a, n):
+            if a == 0 and st["group_first"] == st["first"]:
+                e_sum_of[st["group"]] = tail.tile([P, MAX_GROUP, D_FEAT], F32, name="e_sum", bufs=3)
             if a == 0:
-                st["e_sum"] = tail.tile([P, MAXT, D_FEAT], F32, name="e_sum", bufs=C_BUFS)
+                k = st["first"] - st["group_first"]
+                st["e_sum"] = e_sum_of[st["group"]][:, k : k + st["nt"], :]
             e_sum_ps = psum.tile([P, MAXT, P], F32, name="e_sum_ps", tag="e_sum_ps", bufs=1)
             for i in range(n):
                 for moving, first_of_group in ((ident_f32, True), (swap_f32, False)):
@@ -361,27 +362,23 @@ def tile_variableselectionnetwork_pa_t_kernel(
             nc.scalar.copy(out=st["e_sum"][:, a : a + n, :], in_=e_sum_ps[:, 0:n, 0:D_FEAT])
 
         def invert(group):
-            for st in group:
-                nt = st["nt"]
-                nc.scalar.activation(out=st["e_sum"][:, 0:nt, :], in_=st["e_sum"][:, 0:nt, :], func=ACT.Ln)
-            for st in group:
-                nt = st["nt"]
-                nc.scalar.activation(out=st["e_sum"][:, 0:nt, :], in_=st["e_sum"][:, 0:nt, :], func=ACT.Exp, scale=-1.0)
+            n = sum(st["nt"] for st in group)
+            sums = e_sum_of[group[0]["group"]][:, 0:n, :]
+            nc.scalar.activation(out=sums, in_=sums, func=ACT.Ln)
+            nc.scalar.activation(out=sums, in_=sums, func=ACT.Exp, scale=-1.0)
 
-        def output(st, a):
-            if a == 0:
-                st["out"] = tail.tile([P, MAXT, WIDTH], F32, name="out_sb", bufs=5)
+        def output(st):
+            nt = st["nt"]
+            out_sb = tail.tile([P, MAXT, WIDTH], F32, name="out_sb", bufs=5)
             nc.vector.tensor_tensor(
-                out=by_variable(st["out"][:, a, :]),
-                in0=by_variable(st["c"][:, a, :]),
-                in1=over_variables(st["e_sum"][:, a, :]),
+                out=by_variable(out_sb[:, 0:nt, :]),
+                in0=by_variable(st["c"][:, 0:nt, :]),
+                in1=over_variables(st["e_sum"][:, 0:nt, :]),
                 op=ALU.mult,
             )
-            if a == st["nt"] - 1:
-                nc.sync.dma_start(
-                    out=out[st["rows"], :, :].rearrange("(p a) n d -> p a (n d)", a=st["nt"]),
-                    in_=st["out"][:, 0 : st["nt"], :],
-                )
+            nc.sync.dma_start(
+                out=out[st["rows"], :, :].rearrange("(p a) n d -> p a (n d)", a=nt), in_=out_sb[:, 0:nt, :]
+            )
 
         transpose_h(units[0], 0)
         quantise_h(units[0])
@@ -412,6 +409,10 @@ def tile_variableselectionnetwork_pa_t_kernel(
         group_of = []
         for i, n in enumerate(GROUPS):
             group_of += [i] * n
+        e_sum_of = {}
+        for i, st in enumerate(units):
+            st["group"] = group_of[i]
+            st["group_first"] = units[group_of.index(group_of[i])]["first"]
         for i, st in enumerate(units):
             nt, f = st["nt"], st["first"]
             pair = min(2, nt)
@@ -441,8 +442,7 @@ def tile_variableselectionnetwork_pa_t_kernel(
             t3 = t2 + nt + O_R
             for a in range(nt):
                 at(t3 + a, residual, st, a)
-                if a % pair == pair - 1:
-                    at(t3 + a + O_MEAN, mean, st, a - pair + 1, pair)
+                at(t3 + a + O_MEAN, mean, st, a)
                 at(t3 + a + O_SQ, squares, st, a)
                 at(t3 + a + O_N1, normalise_1, st, a)
                 if a % pair == pair - 1:
@@ -452,8 +452,7 @@ def tile_variableselectionnetwork_pa_t_kernel(
                     b = a - pair + 1
                     for level in range(3):
                         at(t3 + a + O_MAX + 0.3 * level, maximum, st, b, pair, level)
-                    for k in range(b, a + 1):
-                        at(t3 + k + 1 + O_SUB, subtract_max, st, k)
+                    at(t3 + b + 1 + O_SUB, subtract_max, st, b, pair)
                     at(t3 + a + O_EXP, exponentials, st, b, pair)
                     at(t3 + a + O_S1, sums_1, st, b, pair)
                     at(t3 + a + O_S2, sums_2, st, b, pair)
@@ -463,9 +462,8 @@ def tile_variableselectionnetwork_pa_t_kernel(
                 at(t5, invert, group)
                 n = 0
                 for g in group:
-                    for a in range(g["nt"]):
-                        n += 1
-                        at(t5 + O_OUT + n * OUT_RATE, output, g, a)
+                    n += g["nt"]
+                    at(t5 + O_OUT + n * OUT_RATE, output, g)
         with tc.manual_schedule():
             for when, n, what, args in sorted(steps, key=lambda s: (s[0], s[1])):
                 what(*args)

@@ -23,8 +23,8 @@ EPS = 1e-5
 FLOPS = 3 * 2 * B * WIDTH * WIDTH
 
 SIZES = (2,) * 16
-GROUPS = (8, 6, 2)
-C_BUFS = 14
+GROUPS = (5, 5, 4, 2)
+C_BUFS = 16
 MAX_GROUP = 16
 MAXT = 2
 O_T, O_Q, O_M1, O_QE, O_M2, O_G, O_R = -5, -1, 2, 0.5, 2, 0.25, 1
@@ -464,6 +464,5 @@ def tile_variableselectionnetwork_pa_t_kernel(
                 for g in group:
                     n += g["nt"]
                     at(t5 + O_OUT + n * OUT_RATE, output, g)
-        with tc.manual_schedule():
-            for when, n, what, args in sorted(steps, key=lambda s: (s[0], s[1])):
-                what(*args)
+        for when, n, what, args in sorted(steps, key=lambda s: (s[0], s[1])):
+            what(*args)

@@ -359,7 +359,10 @@ def tile_variableselectionnetwork_pa_t_kernel(
                         stop=not first_of_group,
                         is_transpose=True,
                     )
-            nc.scalar.copy(out=st["e_sum"][:, a : a + n, :], in_=e_sum_ps[:, 0:n, 0:D_FEAT])
+            if st["group"] == len(GROUPS) - 1:
+                nc.vector.reciprocal(out=st["e_sum"][:, a : a + n, :], in_=e_sum_ps[:, 0:n, 0:D_FEAT])
+            else:
+                nc.scalar.copy(out=st["e_sum"][:, a : a + n, :], in_=e_sum_ps[:, 0:n, 0:D_FEAT])
 
         def invert(group):
             n = sum(st["nt"] for st in group)
@@ -459,7 +462,8 @@ def tile_variableselectionnetwork_pa_t_kernel(
             if i + 1 == len(units) or group_of[i + 1] != group_of[i]:
                 group = [units[k] for k in range(len(units)) if group_of[k] == group_of[i]]
                 t5 = t3 + nt - 1 + O_S2 + O_INV
-                at(t5, invert, group)
+                if group[0]["group"] < len(GROUPS) - 1:
+                    at(t5, invert, group)
                 n = 0
                 for g in group:
                     n += g["nt"]

@@ -67,12 +67,15 @@ def tile_variableselectionnetwork_pa_t_kernel(
             return raw
 
         load_h(units[0])
-        w1_raw = load_weight(cW1, "w1_raw")
+        w1_raw = setup.tile([P, PACK, WIDTH], BF16, name="w1_raw")
+        for half in range(2):
+            cols = slice(half * WIDTH // 2, (half + 1) * WIDTH // 2)
+            nc.sync.dma_start(out=w1_raw[:, :, cols], in_=cW1[:, cols].rearrange("(p t) c -> p t c", t=PACK))
         cb1_raw = setup.tile([P, PACK], BF16, name="cb1_raw")
         nc.sync.dma_start(out=cb1_raw[:], in_=cb1.rearrange("(p t) -> p t", t=PACK))
-        load_h(units[1])
-        w5_raw = load_weight(cW5, "w5_raw")
+        load_x(units[0])
         w4_raw = load_weight(cW4, "w4_raw")
+        w5_raw = load_weight(cW5, "w5_raw")
         bias_rows = setup.tile([P, P], BF16, name="bias_rows")
         nc.vector.memset(bias_rows[:], 0.0)
         for i, vec in enumerate((cb4, cb5)):
@@ -80,8 +83,8 @@ def tile_variableselectionnetwork_pa_t_kernel(
                 out=bias_rows[FEAT_TILES * i : FEAT_TILES * (i + 1), :],
                 in_=vec.rearrange("(t p) -> t p", p=P),
             )
+        load_h(units[1])
         load_h(units[2])
-        load_x(units[0])
         clng_bc = consts.tile([P, WIDTH], BF16, name="clng_bc")
         nc.sync.dma_start(out=clng_bc[:], in_=clng.partition_broadcast(P))
         clnb_bc = consts.tile([P, WIDTH], BF16, name="clnb_bc")
@@ -102,10 +105,12 @@ def tile_variableselectionnetwork_pa_t_kernel(
         def regroup(raw, copy, name, permute):
             grouped = setup.tile([P, WIDTH, PACK], BF16, name=name + "_grouped", align_bytes=64)
             if permute:
-                copy(
-                    out=grouped[:].rearrange("p (i m) t -> p i m t", i=PACK),
-                    in_=raw[:].rearrange("p t (m i) -> p i m t", i=PACK),
-                )
+                for half in range(2):
+                    m = slice(half * P // 2, (half + 1) * P // 2)
+                    copy(
+                        out=grouped[:].rearrange("p (i m) t -> p i m t", i=PACK)[:, :, m, :],
+                        in_=raw[:].rearrange("p t (m i) -> p i m t", i=PACK)[:, :, m, :],
+                    )
             else:
                 copy(
                     out=grouped[:].rearrange("p (c i) t -> p c t i", i=4),
@@ -123,10 +128,6 @@ def tile_variableselectionnetwork_pa_t_kernel(
             )
             return codes, scales
 
-        w1_grouped = regroup(w1_raw, nc.vector.tensor_copy, "w1", True)
-        w1_codes, w1_scales = quantise_weight(w1_grouped, "w1")
-        cb1_cols = consts.tile([P, PACK], F32, name="cb1_cols")
-        nc.vector.tensor_copy(out=cb1_cols[:], in_=cb1_raw[:])
         def over_variables(per_feature):
             return per_feature.unsqueeze(2).to_broadcast([P, per_feature.shape[1], N_VAR, D_FEAT])
 
@@ -373,36 +374,44 @@ def tile_variableselectionnetwork_pa_t_kernel(
         def output(st):
             nt = st["nt"]
             out_sb = tail.tile([P, MAXT, WIDTH], F32, name="out_sb", bufs=5)
-            nc.vector.tensor_tensor(
-                out=by_variable(out_sb[:, 0:nt, :]),
-                in0=by_variable(st["c"][:, 0:nt, :]),
-                in1=over_variables(st["e_sum"][:, 0:nt, :]),
-                op=ALU.mult,
-            )
-            nc.sync.dma_start(
-                out=out[st["rows"], :, :].rearrange("(p a) n d -> p a (n d)", a=nt), in_=out_sb[:, 0:nt, :]
-            )
+            n = 1 if st is units[-1] else nt
+            for a in range(0, nt, n):
+                nc.vector.tensor_tensor(
+                    out=by_variable(out_sb[:, a : a + n, :]),
+                    in0=by_variable(st["c"][:, a : a + n, :]),
+                    in1=over_variables(st["e_sum"][:, a : a + n, :]),
+                    op=ALU.mult,
+                )
+                nc.sync.dma_start(
+                    out=out[st["rows"], :, :].rearrange("(p a) n d -> p a (n d)", a=nt)[:, a : a + n, :],
+                    in_=out_sb[:, a : a + n, :],
+                )
 
-        transpose_h(units[0], 0)
-        quantise_h(units[0])
-        transpose_h(units[1], 0)
-        w5_grouped = regroup(w5_raw, nc.vector.tensor_copy, "w5", False)
-        w4_grouped = regroup(w4_raw, nc.scalar.copy, "w4", False)
-        swap_f32 = consts.tile([P, P], F32, name="swap_f32")
-        nc.vector.tensor_copy(out=swap_f32[:, 0:D_FEAT], in_=ident_f32[:, D_FEAT:P])
-        nc.vector.tensor_copy(out=swap_f32[:, D_FEAT:P], in_=ident_f32[:, 0:D_FEAT])
-        for a in range(MAXT):
-            first_product(units[0], a)
-        quantise_e1(units[0])
-        w4_codes, w4_scales = quantise_weight(w4_grouped, "w4")
-        w5_codes, w5_scales = quantise_weight(w5_grouped, "w5")
-        bias_ps = psum.tile([P, P], BF16, name="bias_ps", tag="e_sum_ps", bufs=1)
-        nc.tensor.transpose(bias_ps[:], bias_rows[:], ident_bf16[:])
-        half_cb45_cols = consts.tile([P, 2 * FEAT_TILES], F32, name="half_cb45_cols")
-        nc.vector.tensor_scalar_mul(out=half_cb45_cols[:], in0=bias_ps[:, 0 : 2 * FEAT_TILES], scalar1=0.5)
-        half_cb4_cols = half_cb45_cols[:, 0:FEAT_TILES]
-        half_cb5_cols = half_cb45_cols[:, FEAT_TILES : 2 * FEAT_TILES]
-        quantise_h(units[1])
+        with tc.manual_schedule():
+            transpose_h(units[0], 0)
+            w1_grouped = regroup(w1_raw, nc.vector.tensor_copy, "w1", True)
+            quantise_h(units[0])
+            w1_codes, w1_scales = quantise_weight(w1_grouped, "w1")
+            w4_grouped = regroup(w4_raw, nc.scalar.copy, "w4", False)
+            cb1_cols = consts.tile([P, PACK], F32, name="cb1_cols")
+            nc.vector.tensor_copy(out=cb1_cols[:], in_=cb1_raw[:])
+            w5_grouped = regroup(w5_raw, nc.vector.tensor_copy, "w5", False)
+            for a in range(MAXT):
+                first_product(units[0], a)
+            w4_codes, w4_scales = quantise_weight(w4_grouped, "w4")
+            quantise_e1(units[0])
+            w5_codes, w5_scales = quantise_weight(w5_grouped, "w5")
+            bias_ps = psum.tile([P, P], BF16, name="bias_ps", tag="e_sum_ps", bufs=1)
+            nc.tensor.transpose(bias_ps[:], bias_rows[:], ident_bf16[:])
+            half_cb45_cols = consts.tile([P, 2 * FEAT_TILES], F32, name="half_cb45_cols")
+            nc.vector.tensor_scalar_mul(out=half_cb45_cols[:], in0=bias_ps[:, 0 : 2 * FEAT_TILES], scalar1=0.5)
+            half_cb4_cols = half_cb45_cols[:, 0:FEAT_TILES]
+            half_cb5_cols = half_cb45_cols[:, FEAT_TILES : 2 * FEAT_TILES]
+            transpose_h(units[1], 0)
+            quantise_h(units[1])
+            swap_f32 = consts.tile([P, P], F32, name="swap_f32")
+            nc.vector.tensor_copy(out=swap_f32[:, 0:D_FEAT], in_=ident_f32[:, D_FEAT:P])
+            nc.vector.tensor_copy(out=swap_f32[:, D_FEAT:P], in_=ident_f32[:, 0:D_FEAT])
 
         steps = []
 

@@ -20,15 +20,16 @@ D_FEAT = 64
 FEAT_TILES = WIDTH // P
 EPS = 1e-5
 
+UT = 2
+ROWS = UT * P
+N_UNITS = B // ROWS
+LN_GROUPS = (range(0, 5), range(5, 10), range(10, 14))
+LAST_UNITS = range(14, N_UNITS)
+AHEAD = 8
+X_AHEAD = 6
+
 FLOPS = 3 * 2 * B * WIDTH * WIDTH
 
-SIZES = (2,) * 16
-GROUPS = (5, 5, 4, 2)
-C_BUFS = 16
-MAX_GROUP = 16
-MAXT = 2
-O_T, O_Q, O_M1, O_QE, O_M2, O_G, O_R = -5, -1, 2, 0.5, 2, 0.25, 1
-O_MEAN, O_SQ, O_N1, O_N2, O_MAX, O_SUB, O_EXP, O_S1, O_S2, O_INV, O_OUT, OUT_RATE = 0.1, 0.6, 0.7, 3.5, 4, 5, 7, 8.5, 9.5, 1, 0.5, 1
 
 def tile_variableselectionnetwork_pa_t_kernel(
     tc, h, x, cW1, cb1, cW4, cb4, cW5, cb5, clng, clnb, out
@@ -37,29 +38,25 @@ def tile_variableselectionnetwork_pa_t_kernel(
     with ExitStack() as ctx:
         consts = ctx.enter_context(tc.tile_pool(name="consts", bufs=1))
         setup = ctx.enter_context(tc.tile_pool(name="setup", bufs=1))
-        io = ctx.enter_context(tc.tile_pool(name="io", bufs=8))
+        io = ctx.enter_context(tc.tile_pool(name="io", bufs=AHEAD))
         work = ctx.enter_context(tc.tile_pool(name="work", bufs=3))
         gate = ctx.enter_context(tc.tile_pool(name="gate", bufs=2))
         tail = ctx.enter_context(tc.tile_pool(name="tail", bufs=3))
         psum = ctx.enter_context(tc.psum_pool(name="psum", bufs=2))
 
-        units = []
-        for nt in SIZES:
-            first = units[-1]["first"] + units[-1]["nt"] if units else 0
-            units.append({"first": first, "nt": nt, "rows": slice(first * P, (first + nt) * P)})
+        units = [{"rows": slice(u * ROWS, (u + 1) * ROWS)} for u in range(N_UNITS)]
+        sums_of = {}
+        for group in (*LN_GROUPS, LAST_UNITS):
+            for u in group:
+                units[u]["group"] = group
 
         def load_h(st):
-            st["h"] = io.tile([P, MAXT, WIDTH], BF16, name="h_sb")
-            nc.sync.dma_start(
-                out=st["h"][:, 0 : st["nt"], :], in_=h[st["rows"], :].rearrange("(p a) k -> p a k", a=st["nt"])
-            )
+            st["h"] = io.tile([P, UT, WIDTH], BF16, name="h_sb")
+            nc.sync.dma_start(out=st["h"][:], in_=h[st["rows"], :].rearrange("(p a) k -> p a k", a=UT))
 
         def load_x(st):
-            st["x"] = io.tile([P, MAXT, WIDTH], BF16, name="x_sb")
-            nc.sync.dma_start(
-                out=st["x"][:, 0 : st["nt"], :],
-                in_=x[st["rows"], :, :].rearrange("(p a) n d -> p a (n d)", a=st["nt"]),
-            )
+            st["x"] = io.tile([P, UT, WIDTH], BF16, name="x_sb")
+            nc.sync.dma_start(out=st["x"][:], in_=x[st["rows"], :, :].rearrange("(p a) n d -> p a (n d)", a=UT))
 
         def load_weight(w, name):
             raw = setup.tile([P, PACK, WIDTH], BF16, name=name)
@@ -89,33 +86,35 @@ def tile_variableselectionnetwork_pa_t_kernel(
         nc.sync.dma_start(out=clng_bc[:], in_=clng.partition_broadcast(P))
         clnb_bc = consts.tile([P, WIDTH], BF16, name="clnb_bc")
         nc.sync.dma_start(out=clnb_bc[:], in_=clnb.partition_broadcast(P))
-        for i in range(1, 6):
-            load_h(units[i + 2])
-            load_x(units[i])
+        for u in range(1, X_AHEAD):
+            load_h(units[u + AHEAD - X_AHEAD])
+            load_x(units[u])
 
         ident_f32 = consts.tile([P, P], F32, name="ident_f32")
         make_identity(nc, ident_f32[:])
         ident_bf16 = consts.tile([P, P], BF16, name="ident_bf16")
         make_identity(nc, ident_bf16[:])
-        neg_half = consts.tile([P, MAXT], F32, name="neg_half")
+        neg_half = consts.tile([P, UT], F32, name="neg_half")
         nc.vector.memset(neg_half[:], -0.5)
         warm = consts.tile([P, 1], F32, name="warm")
         nc.scalar.activation(out=warm[:], in_=neg_half[:, 0:1], func=ACT.Exp)
 
-        def regroup(raw, copy, name, permute):
-            grouped = setup.tile([P, WIDTH, PACK], BF16, name=name + "_grouped", align_bytes=64)
-            if permute:
-                for half in range(2):
-                    m = slice(half * P // 2, (half + 1) * P // 2)
-                    copy(
-                        out=grouped[:].rearrange("p (i m) t -> p i m t", i=PACK)[:, :, m, :],
-                        in_=raw[:].rearrange("p t (m i) -> p i m t", i=PACK)[:, :, m, :],
-                    )
-            else:
-                copy(
-                    out=grouped[:].rearrange("p (c i) t -> p c t i", i=4),
-                    in_=raw[:].rearrange("p t (c i) -> p c t i", i=4),
+        def regroup_w1():
+            grouped = setup.tile([P, WIDTH, PACK], BF16, name="w1_grouped", align_bytes=64)
+            for half in range(2):
+                m = slice(half * P // 2, (half + 1) * P // 2)
+                nc.vector.tensor_copy(
+                    out=grouped[:].rearrange("p (i m) t -> p i m t", i=PACK)[:, :, m, :],
+                    in_=w1_raw[:].rearrange("p t (m i) -> p i m t", i=PACK)[:, :, m, :],
                 )
+            return grouped
+
+        def regroup(raw, copy, name):
+            grouped = setup.tile([P, WIDTH, PACK], BF16, name=name + "_grouped", align_bytes=64)
+            copy(
+                out=grouped[:].rearrange("p (c i) t -> p c t i", i=4),
+                in_=raw[:].rearrange("p t (c i) -> p c t i", i=4),
+            )
             return grouped
 
         def quantise_weight(grouped, name):
@@ -128,40 +127,28 @@ def tile_variableselectionnetwork_pa_t_kernel(
             )
             return codes, scales
 
-        def over_variables(per_feature):
-            return per_feature.unsqueeze(2).to_broadcast([P, per_feature.shape[1], N_VAR, D_FEAT])
-
-        def by_variable(tile_ap):
-            return tile_ap.rearrange("p a (n d) -> p a n d", n=N_VAR)
-
-        def transpose_h(st, a):
-            nt = st["nt"]
-            if a == 0:
-                st["h_grouped"] = work.tile([P, MAXT * P * PACK], BF16, name="h_grouped", align_bytes=64)
-            n = min(2, nt)
-            hT_ps = psum.tile([P, 2, 2, P], F32, name="hT_ps", tag="hT_ps", bufs=1)
-            for i in range(n):
-                h_words = st["h"][:, a + i, :].bitcast(F32)
+        def transpose_h(st):
+            st["h_grouped"] = work.tile([P, ROWS * PACK], BF16, name="h_grouped", align_bytes=64)
+            hT_ps = psum.tile([P, UT, 2, P], F32, name="hT_ps", tag="hT_ps", bufs=1)
+            for a in range(UT):
+                words = st["h"][:, a, :].bitcast(F32)
                 for w in range(2):
-                    nc.tensor.transpose(hT_ps[:, i, w, :], h_words[:, w : 2 * P : 2], ident_f32[:])
+                    nc.tensor.transpose(hT_ps[:, a, w, :], words[:, w : 2 * P : 2], ident_f32[:])
             nc.scalar.copy(
-                out=st["h_grouped"][:].bitcast(F32).rearrange("q (a b w) -> q a b w", a=MAXT, w=2)[:, a : a + n, :, :],
-                in_=hT_ps[:, 0:n, :, :].rearrange("q a w b -> q a b w"),
+                out=st["h_grouped"][:].bitcast(F32).rearrange("q (a b w) -> q a b w", a=UT, w=2),
+                in_=hT_ps[:].rearrange("q a w b -> q a b w"),
             )
 
         def quantise_h(st):
-            rows = st["nt"] * P
-            st["h_codes"] = work.tile([P, MAXT * P], U32, name="h_codes", align_bytes=64)
-            st["h_scales"] = work.tile([P, MAXT * P], U8, name="h_scales", align_bytes=64)
+            st["h_codes"] = work.tile([P, ROWS], U32, name="h_codes", align_bytes=64)
+            st["h_scales"] = work.tile([P, ROWS], U8, name="h_scales", align_bytes=64)
             nc.vector.quantize_mx(
-                out=st["h_codes"][:, 0:rows].bitcast(FP8X4),
-                scales=st["h_scales"][:, 0:rows],
-                in_=st["h_grouped"][:, 0 : rows * PACK],
+                out=st["h_codes"][:].bitcast(FP8X4), scales=st["h_scales"][:], in_=st["h_grouped"][:]
             )
 
         def first_product(st, a):
             if a == 0:
-                st["e1_grouped"] = work.tile([P, MAXT * P, PACK], BF16, name="e1_grouped", align_bytes=64)
+                st["e1_grouped"] = work.tile([P, ROWS, PACK], BF16, name="e1_grouped", align_bytes=64)
             cols = slice(a * P, (a + 1) * P)
             e1_ps = psum.tile([P, PACK, P], F32, name="e1_ps", tag="e1_ps", bufs=2)
             for t in range(PACK):
@@ -183,46 +170,43 @@ def tile_variableselectionnetwork_pa_t_kernel(
             )
 
         def quantise_e1(st):
-            rows = st["nt"] * P
-            st["e1_codes"] = work.tile([P, MAXT * P], U32, name="e1_codes", align_bytes=64)
-            st["e1_scales"] = work.tile([P, MAXT * P], U8, name="e1_scales", align_bytes=64)
+            st["e1_codes"] = work.tile([P, ROWS], U32, name="e1_codes", align_bytes=64)
+            st["e1_scales"] = work.tile([P, ROWS], U8, name="e1_scales", align_bytes=64)
             nc.vector.quantize_mx(
-                out=st["e1_codes"][:, 0:rows].bitcast(FP8X4),
-                scales=st["e1_scales"][:, 0:rows],
-                in_=st["e1_grouped"][:, 0:rows, :].rearrange("p b t -> p (b t)"),
+                out=st["e1_codes"][:].bitcast(FP8X4),
+                scales=st["e1_scales"][:],
+                in_=st["e1_grouped"][:].rearrange("p b t -> p (b t)"),
             )
 
         def second_product(st, j):
-            rows = st["nt"] * P
             if j == 0:
-                st["tanh"] = gate.tile([P, FEAT_TILES, MAXT * P], F32, name="tanh_sb")
-                st["lin"] = gate.tile([P, FEAT_TILES, MAXT * P], F32, name="half_lin_sb")
+                st["tanh"] = gate.tile([P, FEAT_TILES, ROWS], F32, name="tanh_sb")
+                st["lin"] = gate.tile([P, FEAT_TILES, ROWS], F32, name="half_lin_sb")
             feats = slice(j * P, (j + 1) * P)
-            u_ps = psum.tile([P, 2, MAXT * P], F32, name="u_ps", tag="u_ps", bufs=2)
+            u_ps = psum.tile([P, 2, ROWS], F32, name="u_ps", tag="u_ps", bufs=2)
             for i, codes, scales in ((0, w4_codes, w4_scales), (1, w5_codes, w5_scales)):
                 nc.tensor.matmul_mx(
-                    out=u_ps[:, i, 0:rows],
+                    out=u_ps[:, i, :],
                     lhsT=codes[:, feats].bitcast(FP8X4),
                     lhsT_scale=scales[:, feats],
-                    rhs=st["e1_codes"][:, 0:rows].bitcast(FP8X4),
-                    rhs_scale=st["e1_scales"][:, 0:rows],
+                    rhs=st["e1_codes"][:].bitcast(FP8X4),
+                    rhs_scale=st["e1_scales"][:],
                     start=True,
                     stop=True,
                 )
             for i, dst, func, bias in ((0, "tanh", ACT.Tanh, half_cb4_cols), (1, "lin", ACT.Identity, half_cb5_cols)):
                 nc.scalar.activation(
-                    out=st[dst][:, j, 0:rows], in_=u_ps[:, i, 0:rows], func=func, bias=bias[:, j : j + 1], scale=0.5
+                    out=st[dst][:, j, :], in_=u_ps[:, i, :], func=func, bias=bias[:, j : j + 1], scale=0.5
                 )
 
-        def gate_product(st, j2):
-            rows = st["nt"] * P
-            if j2 == 0:
-                st["gT"] = gate.tile([P, FEAT_TILES, MAXT * P], F32, name="gT")
+        def gate_product(st, j):
+            if j == 0:
+                st["gT"] = gate.tile([P, FEAT_TILES, ROWS], F32, name="gT")
             nc.vector.scalar_tensor_tensor(
-                out=st["gT"][:, j2 : j2 + 2, 0:rows],
-                in0=st["tanh"][:, j2 : j2 + 2, 0:rows],
+                out=st["gT"][:, j : j + 2, :],
+                in0=st["tanh"][:, j : j + 2, :],
                 scalar=1.0,
-                in1=st["lin"][:, j2 : j2 + 2, 0:rows],
+                in1=st["lin"][:, j : j + 2, :],
                 op0=ALU.add,
                 op1=ALU.mult,
             )
@@ -230,7 +214,7 @@ def tile_variableselectionnetwork_pa_t_kernel(
         def residual(st, a):
             if a == 0:
                 st["r"] = []
-                st["neg_mean"] = tail.tile([P, MAXT], F32, name="neg_mean")
+                st["neg_mean"] = tail.tile([P, UT], F32, name="neg_mean")
             r_ps = psum.tile([P, WIDTH], F32, name="r_ps", tag="r_ps", bufs=2)
             st["r"].append(r_ps)
             nc.tensor.matmul(out=r_ps[:], lhsT=ident_bf16[:], rhs=st["x"][:, a, :], start=True, stop=False)
@@ -256,9 +240,9 @@ def tile_variableselectionnetwork_pa_t_kernel(
 
         def squares(st, a):
             if a == 0:
-                st["dev"] = tail.tile([P, MAXT], F32, name="dev_sq_sum")
-                st["var"] = tail.tile([P, MAXT], F32, name="var_eps")
-                st["rstd"] = tail.tile([P, MAXT], F32, name="rstd")
+                st["dev"] = tail.tile([P, UT], F32, name="dev_sq_sum")
+                st["var"] = tail.tile([P, UT], F32, name="var_eps")
+                st["rstd"] = tail.tile([P, UT], F32, name="rstd")
             unused = tail.tile([P, WIDTH], BF16, name="unused", bufs=1)
             nc.scalar.activation(
                 out=unused[:],
@@ -269,22 +253,15 @@ def tile_variableselectionnetwork_pa_t_kernel(
                 accum_out=st["dev"][:, a : a + 1],
             )
 
-        def reciprocal_std(st, a, n):
+        def reciprocal_std(st):
             nc.gpsimd.tensor_scalar(
-                out=st["var"][:, a : a + n],
-                in0=st["dev"][:, a : a + n],
-                scalar1=1.0 / WIDTH,
-                scalar2=EPS,
-                op0=ALU.mult,
-                op1=ALU.add,
+                out=st["var"][:], in0=st["dev"][:], scalar1=1.0 / WIDTH, scalar2=EPS, op0=ALU.mult, op1=ALU.add
             )
-            nc.gpsimd.tensor_tensor(
-                out=st["rstd"][:, a : a + n], in0=st["var"][:, a : a + n], in1=neg_half[:, 0:n], op=ALU.pow
-            )
+            nc.gpsimd.tensor_tensor(out=st["rstd"][:], in0=st["var"][:], in1=neg_half[:], op=ALU.pow)
 
         def normalise_1(st, a):
             if a == 0:
-                st["c"] = tail.tile([P, MAXT, WIDTH], F32, name="c_sb", bufs=C_BUFS)
+                st["c"] = tail.tile([P, UT, WIDTH], F32, name="c_sb", bufs=N_UNITS)
             nc.vector.scalar_tensor_tensor(
                 out=st["c"][:, a, :],
                 in0=st["r"][a][:],
@@ -304,78 +281,78 @@ def tile_variableselectionnetwork_pa_t_kernel(
                 op1=ALU.add,
             )
 
-        def maximum(st, a, n, level):
+        def over_variables(per_feature):
+            return per_feature.unsqueeze(2).to_broadcast([P, per_feature.shape[1], N_VAR, D_FEAT])
+
+        def by_variable(tile_ap):
+            return tile_ap.rearrange("p a (n d) -> p a n d", n=N_VAR)
+
+        def maximum(st, level):
             width = WIDTH >> (level + 1)
-            src = st["max%d" % (level - 1)][:, a : a + n, :] if level else st["c"][:, a : a + n, :]
-            if a == 0:
-                st["max%d" % level] = tail.tile([P, MAXT, width], BF16, name="c_max_%d" % width)
+            src = st["max"] if level else st["c"]
+            st["max"] = tail.tile([P, UT, width], BF16, name="c_max_%d" % width)
             nc.vector.tensor_tensor(
-                out=st["max%d" % level][:, a : a + n, :],
-                in0=src[:, :, 0:width],
-                in1=src[:, :, width : 2 * width],
-                op=ALU.max,
+                out=st["max"][:], in0=src[:, :, 0:width], in1=src[:, :, width : 2 * width], op=ALU.max
             )
 
-        def subtract_max(st, a, n):
+        def subtract_max(st):
             nc.vector.tensor_tensor(
-                out=by_variable(st["c"][:, a : a + n, :]),
-                in0=by_variable(st["c"][:, a : a + n, :]),
-                in1=over_variables(st["max2"][:, a : a + n, :]),
+                out=by_variable(st["c"][:]),
+                in0=by_variable(st["c"][:]),
+                in1=over_variables(st["max"][:]),
                 op=ALU.subtract,
             )
 
-        def exponentials(st, a, n):
-            nc.scalar.activation(out=st["c"][:, a : a + n, :], in_=st["c"][:, a : a + n, :], func=ACT.Exp)
+        def exponentials(st):
+            nc.scalar.activation(out=st["c"][:], in_=st["c"][:], func=ACT.Exp)
 
-        def sums_1(st, a, n):
-            if a == 0:
-                st["e_sumT"] = tail.tile([P, MAXT, P], F32, name="e_sumT", bufs=2)
-            e_sumT_ps = psum.tile([P, MAXT, P], F32, name="e_sumT_ps", tag="e_sum_ps", bufs=1)
-            for i in range(n):
+        def sums_1(st):
+            e_sumT = tail.tile([P, UT, P], F32, name="e_sumT", bufs=2)
+            st["e_sumT"] = e_sumT
+            e_sumT_ps = psum.tile([P, UT, P], F32, name="e_sumT_ps", tag="e_sum_ps", bufs=1)
+            for a in range(UT):
                 for j in range(FEAT_TILES):
                     nc.tensor.matmul(
-                        out=e_sumT_ps[:, i, :],
-                        lhsT=st["c"][:, a + i, j * P : (j + 1) * P],
+                        out=e_sumT_ps[:, a, :],
+                        lhsT=st["c"][:, a, j * P : (j + 1) * P],
                         rhs=ident_f32[:],
                         start=(j == 0),
                         stop=(j == FEAT_TILES - 1),
                         is_transpose=True,
                     )
-            nc.scalar.copy(out=st["e_sumT"][:, a : a + n, :], in_=e_sumT_ps[:, 0:n, :])
+            nc.scalar.copy(out=e_sumT[:], in_=e_sumT_ps[:])
 
-        def sums_2(st, a, n):
-            if a == 0 and st["group_first"] == st["first"]:
-                e_sum_of[st["group"]] = tail.tile([P, MAX_GROUP, D_FEAT], F32, name="e_sum", bufs=3)
-            if a == 0:
-                k = st["first"] - st["group_first"]
-                st["e_sum"] = e_sum_of[st["group"]][:, k : k + st["nt"], :]
-            e_sum_ps = psum.tile([P, MAXT, P], F32, name="e_sum_ps", tag="e_sum_ps", bufs=1)
-            for i in range(n):
-                for moving, first_of_group in ((ident_f32, True), (swap_f32, False)):
+        def sums_2(st, u):
+            group = st["group"]
+            if u == group[0]:
+                sums_of[group[0]] = tail.tile([P, len(LN_GROUPS[0]) * UT, D_FEAT], F32, name="e_sum", bufs=3)
+            k = (u - group[0]) * UT
+            st["e_sum"] = sums_of[group[0]][:, k : k + UT, :]
+            e_sum_ps = psum.tile([P, UT, P], F32, name="e_sum_ps", tag="e_sum_ps", bufs=1)
+            for a in range(UT):
+                for moving, first in ((ident_f32, True), (swap_f32, False)):
                     nc.tensor.matmul(
-                        out=e_sum_ps[:, i, :],
-                        lhsT=st["e_sumT"][:, a + i, :],
+                        out=e_sum_ps[:, a, :],
+                        lhsT=st["e_sumT"][:, a, :],
                         rhs=moving[:],
-                        start=first_of_group,
-                        stop=not first_of_group,
+                        start=first,
+                        stop=not first,
                         is_transpose=True,
                     )
-            if st["group"] == len(GROUPS) - 1:
-                nc.vector.reciprocal(out=st["e_sum"][:, a : a + n, :], in_=e_sum_ps[:, 0:n, 0:D_FEAT])
+            if group is LAST_UNITS:
+                nc.vector.reciprocal(out=st["e_sum"], in_=e_sum_ps[:, :, 0:D_FEAT])
             else:
-                nc.scalar.copy(out=st["e_sum"][:, a : a + n, :], in_=e_sum_ps[:, 0:n, 0:D_FEAT])
+                nc.scalar.copy(out=st["e_sum"], in_=e_sum_ps[:, :, 0:D_FEAT])
 
         def invert(group):
-            n = sum(st["nt"] for st in group)
-            sums = e_sum_of[group[0]["group"]][:, 0:n, :]
+            sums = sums_of[group[0]][:, 0 : len(group) * UT, :]
             nc.scalar.activation(out=sums, in_=sums, func=ACT.Ln)
             nc.scalar.activation(out=sums, in_=sums, func=ACT.Exp, scale=-1.0)
 
         def output(st):
-            nt = st["nt"]
-            out_sb = tail.tile([P, MAXT, WIDTH], F32, name="out_sb", bufs=5)
-            n = 1 if st is units[-1] else nt
-            for a in range(0, nt, n):
+            out_sb = tail.tile([P, UT, WIDTH], F32, name="out_sb", bufs=5)
+            n = 1 if st is units[-1] else UT
+            for a in range(0, UT, n):
                 nc.vector.tensor_tensor(
                     out=by_variable(out_sb[:, a : a + n, :]),
                     in0=by_variable(st["c"][:, a : a + n, :]),
@@ -383,20 +360,20 @@ def tile_variableselectionnetwork_pa_t_kernel(
                     op=ALU.mult,
                 )
                 nc.sync.dma_start(
-                    out=out[st["rows"], :, :].rearrange("(p a) n d -> p a (n d)", a=nt)[:, a : a + n, :],
+                    out=out[st["rows"], :, :].rearrange("(p a) n d -> p a (n d)", a=UT)[:, a : a + n, :],
                     in_=out_sb[:, a : a + n, :],
                 )
 
         with tc.manual_schedule():
-            transpose_h(units[0], 0)
-            w1_grouped = regroup(w1_raw, nc.vector.tensor_copy, "w1", True)
+            transpose_h(units[0])
+            w1_grouped = regroup_w1()
             quantise_h(units[0])
             w1_codes, w1_scales = quantise_weight(w1_grouped, "w1")
-            w4_grouped = regroup(w4_raw, nc.scalar.copy, "w4", False)
+            w4_grouped = regroup(w4_raw, nc.scalar.copy, "w4")
             cb1_cols = consts.tile([P, PACK], F32, name="cb1_cols")
             nc.vector.tensor_copy(out=cb1_cols[:], in_=cb1_raw[:])
-            w5_grouped = regroup(w5_raw, nc.vector.tensor_copy, "w5", False)
-            for a in range(MAXT):
+            w5_grouped = regroup(w5_raw, nc.vector.tensor_copy, "w5")
+            for a in range(UT):
                 first_product(units[0], a)
             w4_codes, w4_scales = quantise_weight(w4_grouped, "w4")
             quantise_e1(units[0])
@@ -407,7 +384,7 @@ def tile_variableselectionnetwork_pa_t_kernel(
             nc.vector.tensor_scalar_mul(out=half_cb45_cols[:], in0=bias_ps[:, 0 : 2 * FEAT_TILES], scalar1=0.5)
             half_cb4_cols = half_cb45_cols[:, 0:FEAT_TILES]
             half_cb5_cols = half_cb45_cols[:, FEAT_TILES : 2 * FEAT_TILES]
-            transpose_h(units[1], 0)
+            transpose_h(units[1])
             quantise_h(units[1])
             swap_f32 = consts.tile([P, P], F32, name="swap_f32")
             nc.vector.tensor_copy(out=swap_f32[:, 0:D_FEAT], in_=ident_f32[:, D_FEAT:P])
@@ -418,64 +395,43 @@ def tile_variableselectionnetwork_pa_t_kernel(
         def at(when, what, *args):
             steps.append((when, len(steps), what, args))
 
-        group_of = []
-        for i, n in enumerate(GROUPS):
-            group_of += [i] * n
-        e_sum_of = {}
-        for i, st in enumerate(units):
-            st["group"] = group_of[i]
-            st["group_first"] = units[group_of.index(group_of[i])]["first"]
-        for i, st in enumerate(units):
-            nt, f = st["nt"], st["first"]
-            pair = min(2, nt)
-            if i > 7:
+        for u, st in enumerate(units):
+            f = u * UT
+            if u >= AHEAD:
                 at(f - 10, load_h, st)
-            if i > 5:
+            if u >= X_AHEAD:
                 at(f - 8, load_x, st)
-            t0 = f + O_T
-            if i > 1:
-                for a in range(0, nt, pair):
-                    at(t0 + a, transpose_h, st, a)
-            t1 = t0 + nt + O_Q
-            if i > 1:
-                at(t1, quantise_h, st)
-            t1 += O_M1
-            if i > 0:
-                for a in range(nt):
-                    at(t1 + a, first_product, st, a)
-            t2 = t1 + nt + O_QE
-            if i > 0:
-                at(t2, quantise_e1, st)
-            t2 += O_M2
+            if u > 1:
+                at(f - 5, transpose_h, st)
+                at(f - 4, quantise_h, st)
+            if u > 0:
+                for a in range(UT):
+                    at(f - 2 + a, first_product, st, a)
+                at(f + 0.5, quantise_e1, st)
             for j in range(FEAT_TILES):
-                at(t2 + j * nt / FEAT_TILES, second_product, st, j)
-            for j2 in (0, 2):
-                at(t2 + (j2 + 2) * nt / FEAT_TILES + O_G, gate_product, st, j2)
-            t3 = t2 + nt + O_R
-            for a in range(nt):
-                at(t3 + a, residual, st, a)
-                at(t3 + a + O_MEAN, mean, st, a)
-                at(t3 + a + O_SQ, squares, st, a)
-                at(t3 + a + O_N1, normalise_1, st, a)
-                if a % pair == pair - 1:
-                    at(t3 + a + O_SQ, reciprocal_std, st, a - pair + 1, pair)
-                at(t3 + a + O_N2, normalise_2, st, a)
-                if a % pair == pair - 1:
-                    b = a - pair + 1
-                    for level in range(3):
-                        at(t3 + a + O_MAX + 0.3 * level, maximum, st, b, pair, level)
-                    at(t3 + b + 1 + O_SUB, subtract_max, st, b, pair)
-                    at(t3 + a + O_EXP, exponentials, st, b, pair)
-                    at(t3 + a + O_S1, sums_1, st, b, pair)
-                    at(t3 + a + O_S2, sums_2, st, b, pair)
-            if i + 1 == len(units) or group_of[i + 1] != group_of[i]:
-                group = [units[k] for k in range(len(units)) if group_of[k] == group_of[i]]
-                t5 = t3 + nt - 1 + O_S2 + O_INV
-                if group[0]["group"] < len(GROUPS) - 1:
-                    at(t5, invert, group)
-                n = 0
-                for g in group:
-                    n += g["nt"]
-                    at(t5 + O_OUT + n * OUT_RATE, output, g)
-        for when, n, what, args in sorted(steps, key=lambda s: (s[0], s[1])):
-            what(*args)
+                at(f + 2.5 + j * UT / FEAT_TILES, second_product, st, j)
+            for j in range(0, FEAT_TILES, 2):
+                at(f + 2.75 + (j + 2) * UT / FEAT_TILES, gate_product, st, j)
+            for a in range(UT):
+                at(f + 5.5 + a, residual, st, a)
+                at(f + 5.6 + a, mean, st, a)
+                at(f + 6.1 + a, squares, st, a)
+                at(f + 6.2 + a, normalise_1, st, a)
+            at(f + 7.1, reciprocal_std, st)
+            for a in range(UT):
+                at(f + 9 + a, normalise_2, st, a)
+            for level in range(3):
+                at(f + 10.5 + 0.3 * level, maximum, st, level)
+            at(f + 11.5, subtract_max, st)
+            at(f + 13.5, exponentials, st)
+            at(f + 15, sums_1, st)
+            at(f + 16, sums_2, st, u)
+            group = st["group"]
+            if u == group[-1]:
+                if group is not LAST_UNITS:
+                    at(f + 17, invert, group)
+                for k, v in enumerate(group):
+                    at(f + 19.5 + k * UT, output, units[v])
+        with tc.manual_schedule(engines={mybir.EngineType.PE}):
+            for when, n, what, args in sorted(steps, key=lambda step: step[:2]):
+                what(*args)

from contextlib import ExitStack

import concourse.mybir as mybir
from concourse.masks import make_identity

F32 = mybir.dt.float32
BF16 = mybir.dt.bfloat16
U32 = mybir.dt.uint32
U8 = mybir.dt.uint8
FP8X4 = mybir.dt.float8_e4m3fn_x4
ALU = mybir.AluOpType
ACT = mybir.ActivationFunctionType

P = 128
PACK = 4
B = 4096
WIDTH = 512
N_VAR = 8
D_FEAT = 64
FEAT_TILES = WIDTH // P
EPS = 1e-5

UT = 2
ROWS = UT * P
N_UNITS = B // ROWS
LN_GROUPS = (range(0, 5), range(5, 10), range(10, 14))
LAST_UNITS = range(14, N_UNITS)
AHEAD = 8
X_AHEAD = 6

FLOPS = 3 * 2 * B * WIDTH * WIDTH


def tile_variableselectionnetwork_pa_t_kernel(
    tc, h, x, cW1, cb1, cW4, cb4, cW5, cb5, clng, clnb, out
):
    nc = tc.nc
    with ExitStack() as ctx:
        consts = ctx.enter_context(tc.tile_pool(name="consts", bufs=1))
        setup = ctx.enter_context(tc.tile_pool(name="setup", bufs=1))
        io = ctx.enter_context(tc.tile_pool(name="io", bufs=AHEAD))
        work = ctx.enter_context(tc.tile_pool(name="work", bufs=3))
        gate = ctx.enter_context(tc.tile_pool(name="gate", bufs=2))
        tail = ctx.enter_context(tc.tile_pool(name="tail", bufs=3))
        psum = ctx.enter_context(tc.psum_pool(name="psum", bufs=2))

        units = [{"rows": slice(u * ROWS, (u + 1) * ROWS)} for u in range(N_UNITS)]
        sums_of = {}
        for group in (*LN_GROUPS, LAST_UNITS):
            for u in group:
                units[u]["group"] = group

        def load_h(st):
            st["h"] = io.tile([P, UT, WIDTH], BF16, name="h_sb")
            nc.sync.dma_start(out=st["h"][:], in_=h[st["rows"], :].rearrange("(p a) k -> p a k", a=UT))

        def load_x(st):
            st["x"] = io.tile([P, UT, WIDTH], BF16, name="x_sb")
            nc.sync.dma_start(out=st["x"][:], in_=x[st["rows"], :, :].rearrange("(p a) n d -> p a (n d)", a=UT))

        def load_weight(w, name):
            raw = setup.tile([P, PACK, WIDTH], BF16, name=name)
            nc.sync.dma_start(out=raw[:], in_=w.rearrange("(p t) c -> p t c", t=PACK))
            return raw

        load_h(units[0])
        w1_raw = setup.tile([P, PACK, WIDTH], BF16, name="w1_raw")
        for half in range(2):
            cols = slice(half * WIDTH // 2, (half + 1) * WIDTH // 2)
            nc.sync.dma_start(out=w1_raw[:, :, cols], in_=cW1[:, cols].rearrange("(p t) c -> p t c", t=PACK))
        cb1_raw = setup.tile([P, PACK], BF16, name="cb1_raw")
        nc.sync.dma_start(out=cb1_raw[:], in_=cb1.rearrange("(p t) -> p t", t=PACK))
        load_x(units[0])
        w4_raw = load_weight(cW4, "w4_raw")
        w5_raw = load_weight(cW5, "w5_raw")
        bias_rows = setup.tile([P, P], BF16, name="bias_rows")
        nc.vector.memset(bias_rows[:], 0.0)
        for i, vec in enumerate((cb4, cb5)):
            nc.sync.dma_start(
                out=bias_rows[FEAT_TILES * i : FEAT_TILES * (i + 1), :],
                in_=vec.rearrange("(t p) -> t p", p=P),
            )
        load_h(units[1])
        load_h(units[2])
        clng_bc = consts.tile([P, WIDTH], BF16, name="clng_bc")
        nc.sync.dma_start(out=clng_bc[:], in_=clng.partition_broadcast(P))
        clnb_bc = consts.tile([P, WIDTH], BF16, name="clnb_bc")
        nc.sync.dma_start(out=clnb_bc[:], in_=clnb.partition_broadcast(P))
        for u in range(1, X_AHEAD):
            load_h(units[u + AHEAD - X_AHEAD])
            load_x(units[u])

        ident_f32 = consts.tile([P, P], F32, name="ident_f32")
        make_identity(nc, ident_f32[:])
        ident_bf16 = consts.tile([P, P], BF16, name="ident_bf16")
        make_identity(nc, ident_bf16[:])
        neg_half = consts.tile([P, UT], F32, name="neg_half")
        nc.vector.memset(neg_half[:], -0.5)
        warm = consts.tile([P, 1], F32, name="warm")
        nc.scalar.activation(out=warm[:], in_=neg_half[:, 0:1], func=ACT.Exp)

        def regroup_w1():
            grouped = setup.tile([P, WIDTH, PACK], BF16, name="w1_grouped", align_bytes=64)
            for half in range(2):
                m = slice(half * P // 2, (half + 1) * P // 2)
                nc.vector.tensor_copy(
                    out=grouped[:].rearrange("p (i m) t -> p i m t", i=PACK)[:, :, m, :],
                    in_=w1_raw[:].rearrange("p t (m i) -> p i m t", i=PACK)[:, :, m, :],
                )
            return grouped

        def regroup(raw, copy, name):
            grouped = setup.tile([P, WIDTH, PACK], BF16, name=name + "_grouped", align_bytes=64)
            copy(
                out=grouped[:].rearrange("p (c i) t -> p c t i", i=4),
                in_=raw[:].rearrange("p t (c i) -> p c t i", i=4),
            )
            return grouped

        def quantise_weight(grouped, name):
            codes = consts.tile([P, WIDTH], U32, name=name + "_codes", align_bytes=64)
            scales = consts.tile([P, WIDTH], U8, name=name + "_scales", align_bytes=64)
            nc.vector.quantize_mx(
                out=codes[:].bitcast(FP8X4),
                scales=scales[:],
                in_=grouped[:].rearrange("p c t -> p (c t)"),
            )
            return codes, scales

        def transpose_h(st):
            st["h_grouped"] = work.tile([P, ROWS * PACK], BF16, name="h_grouped", align_bytes=64)
            hT_ps = psum.tile([P, UT, 2, P], F32, name="hT_ps", tag="hT_ps", bufs=1)
            for a in range(UT):
                words = st["h"][:, a, :].bitcast(F32)
                for w in range(2):
                    nc.tensor.transpose(hT_ps[:, a, w, :], words[:, w : 2 * P : 2], ident_f32[:])
            nc.scalar.copy(
                out=st["h_grouped"][:].bitcast(F32).rearrange("q (a b w) -> q a b w", a=UT, w=2),
                in_=hT_ps[:].rearrange("q a w b -> q a b w"),
            )

        def quantise_h(st):
            st["h_codes"] = work.tile([P, ROWS], U32, name="h_codes", align_bytes=64)
            st["h_scales"] = work.tile([P, ROWS], U8, name="h_scales", align_bytes=64)
            nc.vector.quantize_mx(
                out=st["h_codes"][:].bitcast(FP8X4), scales=st["h_scales"][:], in_=st["h_grouped"][:]
            )

        def first_product(st, a):
            if a == 0:
                st["e1_grouped"] = work.tile([P, ROWS, PACK], BF16, name="e1_grouped", align_bytes=64)
            cols = slice(a * P, (a + 1) * P)
            e1_ps = psum.tile([P, PACK, P], F32, name="e1_ps", tag="e1_ps", bufs=2)
            for t in range(PACK):
                feats = slice(t * P, (t + 1) * P)
                nc.tensor.matmul_mx(
                    out=e1_ps[:, t, :],
                    lhsT=w1_codes[:, feats].bitcast(FP8X4),
                    lhsT_scale=w1_scales[:, feats],
                    rhs=st["h_codes"][:, cols].bitcast(FP8X4),
                    rhs_scale=st["h_scales"][:, cols],
                    start=True,
                    stop=True,
                )
            nc.vector.tensor_tensor(
                out=st["e1_grouped"][:, cols, :],
                in0=e1_ps[:].rearrange("p t b -> p b t"),
                in1=cb1_cols[:].unsqueeze(1).to_broadcast([P, P, PACK]),
                op=ALU.add,
            )

        def quantise_e1(st):
            st["e1_codes"] = work.tile([P, ROWS], U32, name="e1_codes", align_bytes=64)
            st["e1_scales"] = work.tile([P, ROWS], U8, name="e1_scales", align_bytes=64)
            nc.vector.quantize_mx(
                out=st["e1_codes"][:].bitcast(FP8X4),
                scales=st["e1_scales"][:],
                in_=st["e1_grouped"][:].rearrange("p b t -> p (b t)"),
            )

        def second_product(st, j):
            if j == 0:
                st["tanh"] = gate.tile([P, FEAT_TILES, ROWS], F32, name="tanh_sb")
                st["lin"] = gate.tile([P, FEAT_TILES, ROWS], F32, name="half_lin_sb")
            feats = slice(j * P, (j + 1) * P)
            u_ps = psum.tile([P, 2, ROWS], F32, name="u_ps", tag="u_ps", bufs=2)
            for i, codes, scales in ((0, w4_codes, w4_scales), (1, w5_codes, w5_scales)):
                nc.tensor.matmul_mx(
                    out=u_ps[:, i, :],
                    lhsT=codes[:, feats].bitcast(FP8X4),
                    lhsT_scale=scales[:, feats],
                    rhs=st["e1_codes"][:].bitcast(FP8X4),
                    rhs_scale=st["e1_scales"][:],
                    start=True,
                    stop=True,
                )
            for i, dst, func, bias in ((0, "tanh", ACT.Tanh, half_cb4_cols), (1, "lin", ACT.Identity, half_cb5_cols)):
                nc.scalar.activation(
                    out=st[dst][:, j, :], in_=u_ps[:, i, :], func=func, bias=bias[:, j : j + 1], scale=0.5
                )

        def gate_product(st, j):
            if j == 0:
                st["gT"] = gate.tile([P, FEAT_TILES, ROWS], F32, name="gT")
            nc.vector.scalar_tensor_tensor(
                out=st["gT"][:, j : j + 2, :],
                in0=st["tanh"][:, j : j + 2, :],
                scalar=1.0,
                in1=st["lin"][:, j : j + 2, :],
                op0=ALU.add,
                op1=ALU.mult,
            )

        def residual(st, a):
            if a == 0:
                st["r"] = []
                st["neg_mean"] = tail.tile([P, UT], F32, name="neg_mean")
            r_ps = psum.tile([P, WIDTH], F32, name="r_ps", tag="r_ps", bufs=2)
            st["r"].append(r_ps)
            nc.tensor.matmul(out=r_ps[:], lhsT=ident_bf16[:], rhs=st["x"][:, a, :], start=True, stop=False)
            for j in range(FEAT_TILES):
                nc.tensor.matmul(
                    out=r_ps[:, j * P : (j + 1) * P],
                    lhsT=st["gT"][:, j, a * P : (a + 1) * P],
                    rhs=ident_f32[:],
                    start=False,
                    stop=(j == FEAT_TILES - 1),
                    is_transpose=True,
                )

        def mean(st, a):
            unused = tail.tile([P, WIDTH], BF16, name="unused", bufs=1)
            nc.scalar.activation(
                out=unused[:],
                in_=st["r"][a][:],
                func=ACT.Identity,
                scale=-1.0 / WIDTH,
                accum_out=st["neg_mean"][:, a : a + 1],
            )

        def squares(st, a):
            if a == 0:
                st["dev"] = tail.tile([P, UT], F32, name="dev_sq_sum")
                st["var"] = tail.tile([P, UT], F32, name="var_eps")
                st["rstd"] = tail.tile([P, UT], F32, name="rstd")
            unused = tail.tile([P, WIDTH], BF16, name="unused", bufs=1)
            nc.scalar.activation(
                out=unused[:],
                in_=st["r"][a][:],
                func=ACT.Square,
                bias=st["neg_mean"][:, a : a + 1],
                scale=1.0,
                accum_out=st["dev"][:, a : a + 1],
            )

        def reciprocal_std(st):
            nc.gpsimd.tensor_scalar(
                out=st["var"][:], in0=st["dev"][:], scalar1=1.0 / WIDTH, scalar2=EPS, op0=ALU.mult, op1=ALU.add
            )
            nc.gpsimd.tensor_tensor(out=st["rstd"][:], in0=st["var"][:], in1=neg_half[:], op=ALU.pow)

        def normalise_1(st, a):
            if a == 0:
                st["c"] = tail.tile([P, UT, WIDTH], F32, name="c_sb", bufs=N_UNITS)
            nc.vector.scalar_tensor_tensor(
                out=st["c"][:, a, :],
                in0=st["r"][a][:],
                scalar=st["neg_mean"][:, a : a + 1],
                in1=clng_bc[:],
                op0=ALU.add,
                op1=ALU.mult,
            )

        def normalise_2(st, a):
            nc.vector.scalar_tensor_tensor(
                out=st["c"][:, a, :],
                in0=st["c"][:, a, :],
                scalar=st["rstd"][:, a : a + 1],
                in1=clnb_bc[:],
                op0=ALU.mult,
                op1=ALU.add,
            )

        def over_variables(per_feature):
            return per_feature.unsqueeze(2).to_broadcast([P, per_feature.shape[1], N_VAR, D_FEAT])

        def by_variable(tile_ap):
            return tile_ap.rearrange("p a (n d) -> p a n d", n=N_VAR)

        def maximum(st, level):
            width = WIDTH >> (level + 1)
            src = st["max"] if level else st["c"]
            st["max"] = tail.tile([P, UT, width], BF16, name="c_max_%d" % width)
            nc.vector.tensor_tensor(
                out=st["max"][:], in0=src[:, :, 0:width], in1=src[:, :, width : 2 * width], op=ALU.max
            )

        def subtract_max(st):
            nc.vector.tensor_tensor(
                out=by_variable(st["c"][:]),
                in0=by_variable(st["c"][:]),
                in1=over_variables(st["max"][:]),
                op=ALU.subtract,
            )

        def exponentials(st):
            nc.scalar.activation(out=st["c"][:], in_=st["c"][:], func=ACT.Exp)

        def sums_1(st):
            e_sumT = tail.tile([P, UT, P], F32, name="e_sumT", bufs=2)
            st["e_sumT"] = e_sumT
            e_sumT_ps = psum.tile([P, UT, P], F32, name="e_sumT_ps", tag="e_sum_ps", bufs=1)
            for a in range(UT):
                for j in range(FEAT_TILES):
                    nc.tensor.matmul(
                        out=e_sumT_ps[:, a, :],
                        lhsT=st["c"][:, a, j * P : (j + 1) * P],
                        rhs=ident_f32[:],
                        start=(j == 0),
                        stop=(j == FEAT_TILES - 1),
                        is_transpose=True,
                    )
            nc.scalar.copy(out=e_sumT[:], in_=e_sumT_ps[:])

        def sums_2(st, u):
            group = st["group"]
            if u == group[0]:
                sums_of[group[0]] = tail.tile([P, len(LN_GROUPS[0]) * UT, D_FEAT], F32, name="e_sum", bufs=3)
            k = (u - group[0]) * UT
            st["e_sum"] = sums_of[group[0]][:, k : k + UT, :]
            e_sum_ps = psum.tile([P, UT, P], F32, name="e_sum_ps", tag="e_sum_ps", bufs=1)
            for a in range(UT):
                for moving, first in ((ident_f32, True), (swap_f32, False)):
                    nc.tensor.matmul(
                        out=e_sum_ps[:, a, :],
                        lhsT=st["e_sumT"][:, a, :],
                        rhs=moving[:],
                        start=first,
                        stop=not first,
                        is_transpose=True,
                    )
            if group is LAST_UNITS:
                nc.vector.reciprocal(out=st["e_sum"], in_=e_sum_ps[:, :, 0:D_FEAT])
            else:
                nc.scalar.copy(out=st["e_sum"], in_=e_sum_ps[:, :, 0:D_FEAT])

        def invert(group):
            sums = sums_of[group[0]][:, 0 : len(group) * UT, :]
            nc.scalar.activation(out=sums, in_=sums, func=ACT.Ln)
            nc.scalar.activation(out=sums, in_=sums, func=ACT.Exp, scale=-1.0)

        def output(st):
            out_sb = tail.tile([P, UT, WIDTH], F32, name="out_sb", bufs=5)
            n = 1 if st is units[-1] else UT
            for a in range(0, UT, n):
                nc.vector.tensor_tensor(
                    out=by_variable(out_sb[:, a : a + n, :]),
                    in0=by_variable(st["c"][:, a : a + n, :]),
                    in1=over_variables(st["e_sum"][:, a : a + n, :]),
                    op=ALU.mult,
                )
                nc.sync.dma_start(
                    out=out[st["rows"], :, :].rearrange("(p a) n d -> p a (n d)", a=UT)[:, a : a + n, :],
                    in_=out_sb[:, a : a + n, :],
                )

        with tc.manual_schedule():
            transpose_h(units[0])
            w1_grouped = regroup_w1()
            quantise_h(units[0])
            w1_codes, w1_scales = quantise_weight(w1_grouped, "w1")
            w4_grouped = regroup(w4_raw, nc.scalar.copy, "w4")
            cb1_cols = consts.tile([P, PACK], F32, name="cb1_cols")
            nc.vector.tensor_copy(out=cb1_cols[:], in_=cb1_raw[:])
            w5_grouped = regroup(w5_raw, nc.vector.tensor_copy, "w5")
            for a in range(UT):
                first_product(units[0], a)
            w4_codes, w4_scales = quantise_weight(w4_grouped, "w4")
            quantise_e1(units[0])
            w5_codes, w5_scales = quantise_weight(w5_grouped, "w5")
            bias_ps = psum.tile([P, P], BF16, name="bias_ps", tag="e_sum_ps", bufs=1)
            nc.tensor.transpose(bias_ps[:], bias_rows[:], ident_bf16[:])
            half_cb45_cols = consts.tile([P, 2 * FEAT_TILES], F32, name="half_cb45_cols")
            nc.vector.tensor_scalar_mul(out=half_cb45_cols[:], in0=bias_ps[:, 0 : 2 * FEAT_TILES], scalar1=0.5)
            half_cb4_cols = half_cb45_cols[:, 0:FEAT_TILES]
            half_cb5_cols = half_cb45_cols[:, FEAT_TILES : 2 * FEAT_TILES]
            transpose_h(units[1])
            quantise_h(units[1])
            swap_f32 = consts.tile([P, P], F32, name="swap_f32")
            nc.vector.tensor_copy(out=swap_f32[:, 0:D_FEAT], in_=ident_f32[:, D_FEAT:P])
            nc.vector.tensor_copy(out=swap_f32[:, D_FEAT:P], in_=ident_f32[:, 0:D_FEAT])

        steps = []

        def at(when, what, *args):
            steps.append((when, len(steps), what, args))

        for u, st in enumerate(units):
            f = u * UT
            if u >= AHEAD:
                at(f - 10, load_h, st)
            if u >= X_AHEAD:
                at(f - 8, load_x, st)
            if u > 1:
                at(f - 5, transpose_h, st)
                at(f - 4, quantise_h, st)
            if u > 0:
                for a in range(UT):
                    at(f - 2 + a, first_product, st, a)
                at(f + 0.5, quantise_e1, st)
            for j in range(FEAT_TILES):
                at(f + 2.5 + j * UT / FEAT_TILES, second_product, st, j)
            for j in range(0, FEAT_TILES, 2):
                at(f + 2.75 + (j + 2) * UT / FEAT_TILES, gate_product, st, j)
            for a in range(UT):
                at(f + 5.5 + a, residual, st, a)
                at(f + 5.6 + a, mean, st, a)
                at(f + 6.1 + a, squares, st, a)
                at(f + 6.2 + a, normalise_1, st, a)
            at(f + 7.1, reciprocal_std, st)
            for a in range(UT):
                at(f + 9 + a, normalise_2, st, a)
            for level in range(3):
                at(f + 10.5 + 0.3 * level, maximum, st, level)
            at(f + 11.5, subtract_max, st)
            at(f + 13.5, exponentials, st)
            at(f + 15, sums_1, st)
            at(f + 16, sums_2, st, u)
            group = st["group"]
            if u == group[-1]:
                if group is not LAST_UNITS:
                    at(f + 17, invert, group)
                for k, v in enumerate(group):
                    at(f + 19.5 + k * UT, output, units[v])
        with tc.manual_schedule(engines={mybir.EngineType.PE}):
            for when, n, what, args in sorted(steps, key=lambda step: step[:2]):
                what(*args)
